import numpy as np
import ml_dtypes


def mxq(x, axis, fmt="e4m3"):
    dtype, down = {"e4m3": (ml_dtypes.float8_e4m3fn, 7), "e5m2": (ml_dtypes.float8_e5m2, 14)}[fmt]
    v = np.moveaxis(np.asarray(x, np.float32).astype(ml_dtypes.bfloat16).astype(np.float64), axis, -1)
    blocks = v.reshape(v.shape[:-1] + (-1, 32))
    amax = np.abs(blocks).max(-1, keepdims=True)
    byte = np.maximum(np.where(amax > 0, np.frexp(amax)[1] - 1 + 127, 0) - down, 1)
    scale = np.exp2(byte - 127.0)
    codes = (blocks / scale).astype(np.float32).astype(dtype).astype(np.float64)
    return np.moveaxis((codes * scale).reshape(v.shape), -1, axis)


WIDE = False


def mx_kscale(k):
    if not WIDE:
        return np.ones(k)
    levels = np.array([10, -10, 5, -5, 0])
    a = np.random.permutation(np.resize(levels, k // 512 * 4)).reshape(k // 512, 4)
    idx = np.arange(k)
    return np.exp2(a[idx // 512, idx % 128 // 32])


BF16 = ml_dtypes.bfloat16


def bf(x):
    return np.asarray(x, np.float32).astype(BF16)


def f64(x):
    return np.asarray(x).astype(np.float64)


E2M1 = np.array([0.0, 0.5, 1.0, 1.5, 2.0, 3.0, 4.0, 6.0, -0.0, -0.5, -1.0, -1.5, -2.0, -3.0, -4.0, -6.0])


def pack_weight(w, fmt):
    k, n = w.shape
    w = f64(bf(w)).reshape(k // 32, 32, n)
    amax = np.abs(w).max(1)
    if fmt == "e4m3":
        byte = np.frexp(amax)[1] - 1 + 127 - 7
    else:
        mant, ex = np.frexp(amax / 6.0)
        byte = np.where(mant > 0.5, ex, ex - 1) + 127
    byte = np.clip(np.where(amax > 0, byte, 1), 1, 254)
    scaled = (w * np.exp2(127.0 - byte)[:, None, :]).reshape(k, n).astype(np.float32)
    by_word = np.ascontiguousarray(scaled.reshape(k // 512, 128, 4, n).transpose(0, 1, 3, 2))
    if fmt == "e4m3":
        words = by_word.astype(ml_dtypes.float8_e4m3fn).view(np.uint8)
    else:
        c = by_word.astype(ml_dtypes.float4_e2m1fn).view(np.uint8) & 0xF
        words = c[..., 0::2] | (c[..., 1::2] << 4)
    return np.ascontiguousarray(words), np.ascontiguousarray(byte.astype(np.uint8).reshape(k // 512, 16, n))


def unpack_weight(words, scales, fmt):
    g, p, n, _ = words.shape
    if fmt == "e4m3":
        vals = np.ascontiguousarray(words).view(ml_dtypes.float8_e4m3fn).astype(np.float64)
    else:
        nib = np.empty((g, p, n, 4), np.uint8)
        nib[..., 0::2] = words & 0xF
        nib[..., 1::2] = words >> 4
        vals = E2M1[nib]
    vals = vals * np.repeat(np.exp2(scales.astype(np.float64) - 127.0), 8, axis=1)[..., None]
    return vals.transpose(0, 1, 3, 2).reshape(g * 512, n)


B, C, HH, WW, D, MH, MW, F, G = 8, 1024, 32, 32, 128, 32, 16, 512, 64
N = B * HH * WW
EPS = 1e-12
VT = 0.5
PA = 3.0
FMT = "e4m3"


def l2norm(v):
    return v / np.maximum(np.sqrt(np.sum(v * v, axis=-1, keepdims=True)), EPS)


def setup_inputs():
    t = mx_kscale(F)
    gp = PA / (PA + np.arange(D))
    z = bf(np.random.standard_normal((B, C, HH, WW)) * (0.5 + np.random.random((B, 1, HH, WW))))
    Wq1_words, Wq1_scales = pack_weight(np.random.standard_normal((C, F)) * t, FMT)
    bq1 = bf(np.random.standard_normal(F) * 0.1 * t)
    Wq2_words, Wq2_scales = pack_weight(np.random.standard_normal((F, D)) * gp * np.sqrt(VT * D / (0.5 * F * np.sum(gp * gp))) / t[:, None], FMT)
    bq2 = bf(np.random.standard_normal(D) * 0.1)
    return {"z": z,
            "Wq1_words": Wq1_words,
            "Wq1_scales": Wq1_scales,
            "bq1": bq1,
            "Wq2_words": Wq2_words,
            "Wq2_scales": Wq2_scales,
            "bq2": bq2}


def reference(z, Wq1_words, Wq1_scales, bq1, Wq2_words, Wq2_scales, bq2):
    x = f64(z).transpose(0, 2, 3, 1).reshape(N, C)
    xn = l2norm(x)
    h = np.maximum((mxq(xn, 1, "e4m3") @ unpack_weight(Wq1_words, Wq1_scales, FMT)) + f64(bq1), 0.0)
    Zq = (mxq(h, 1, "e4m3") @ unpack_weight(Wq2_words, Wq2_scales, FMT)) + f64(bq2)
    mu_z = Zq.mean(axis=1, keepdims=True)
    var_z = Zq.var(axis=1, ddof=1, keepdims=True)
    Zc = l2norm(Zq - mu_z)
    return Zc, var_z

@@ -1,0 +1,361 @@
+from contextlib import ExitStack
+
+import concourse.mybir as mybir
+from concourse.masks import make_identity
+
+BF16 = mybir.dt.bfloat16
+F32 = mybir.dt.float32
+I32 = mybir.dt.int32
+U8 = mybir.dt.uint8
+U32 = mybir.dt.uint32
+FP8X4 = mybir.dt.float8_e4m3fn_x4
+ACT = mybir.ActivationFunctionType
+ALU = mybir.AluOpType
+
+P = 128
+PACK = 4
+BATCH, CHANNELS, PIXELS = 8, 1024, 1024
+HIDDEN, CODE = 512, 128
+PASSES = CHANNELS // (P * PACK)
+CHUNK = 512
+TILES = CHUNK // P
+CHUNKS = BATCH * PIXELS // CHUNK
+EPS = 1e-12
+
+FLOPS = 2 * BATCH * PIXELS * (CHANNELS * HIDDEN + HIDDEN * CODE)
+
+
+TOKEN_TILES = BATCH * PIXELS // P
+BATCH_CHUNKS = PIXELS // CHUNK
+Z_BUFFERS = 3
+
+TILE_SQUARES = 1
+CHUNK_ROOT = 2
+CHUNK_SCALE = 3
+CHUNK_QUANTISE_X = 5
+TILE_PRODUCT_1 = 9
+TILE_BIAS = 10
+TILE_TRANSPOSE_H = 11
+TILE_RELU = 12
+CHUNK_QUANTISE_H = 13
+CHUNK_PRODUCT_2 = 15
+CHUNK_CENTRE = 18
+CHUNK_DEVIATIONS = 19
+CHUNK_DEVIATION_ROOT = 20
+CHUNK_NORMALISE = 21
+STEPS = TOKEN_TILES + CHUNK_NORMALISE
+
+
+def tile_due(step, lag):
+    k = step - lag
+    return k if 0 <= k < TOKEN_TILES else None
+
+
+def chunk_due(step, lag):
+    k = tile_due(step, lag)
+    return k // TILES if k is not None and k % TILES == TILES - 1 else None
+
+
+def load_scale_rows(nc, planes, scales):
+    for quadrant in range(4):
+        nc.sync.dma_start(
+            out=planes[32 * quadrant : 32 * quadrant + 4].bitcast(I32),
+            in_=scales[:, 4 * quadrant : 4 * quadrant + 4, :].rearrange("g r n -> r g n").bitcast(I32),
+        )
+
+
+def tile_spatialmemorymodule_pb_kernel(
+    tc, z, Wq1_words, Wq1_scales, bq1, Wq2_words, Wq2_scales, bq2, out_0, out_1
+):
+    nc = tc.nc
+    with ExitStack() as stack:
+        stack.enter_context(tc.manual_schedule())
+        const = stack.enter_context(tc.tile_pool(name="const", bufs=1))
+        z_pool = stack.enter_context(tc.tile_pool(name="z", bufs=Z_BUFFERS))
+        scrap = stack.enter_context(tc.tile_pool(name="scrap", bufs=4))
+        small = stack.enter_context(tc.tile_pool(name="small", bufs=4))
+        stage = stack.enter_context(tc.tile_pool(name="stage", bufs=4))
+        packed = stack.enter_context(tc.tile_pool(name="packed", bufs=3))
+        result = stack.enter_context(tc.tile_pool(name="result", bufs=3))
+        psum_x = stack.enter_context(tc.psum_pool(name="psum_x", bufs=2))
+        psum_r = stack.enter_context(tc.psum_pool(name="psum_r", bufs=1))
+        psum_h = stack.enter_context(tc.psum_pool(name="psum_h", bufs=2))
+        psum_t = stack.enter_context(tc.psum_pool(name="psum_t", bufs=2))
+        psum_z = stack.enter_context(tc.psum_pool(name="psum_z", bufs=1))
+
+        z_sb = {}
+
+        def load_batch(b):
+            z_sb[b] = z_pool.tile([P, PASSES, PACK, PIXELS], BF16, name="z_sb")
+            for g in range(PASSES):
+                rows = z[b, g * P * PACK : (g + 1) * P * PACK]
+                nc.sync.dma_start(out=z_sb[b][:, g], in_=rows.rearrange("(p t) h w -> p t (h w)", t=PACK))
+
+        load_batch(0)
+
+        ident_bf = const.tile([P, P], BF16)
+        make_identity(nc, ident_bf[:])
+        ident_f32 = const.tile([P, P], F32)
+        make_identity(nc, ident_f32[:])
+
+        w1_words = const.tile([P, PASSES, PACK * HIDDEN], U8, align_bytes=64)
+        w1_planes = const.tile([P, PASSES, HIDDEN], U8, align_bytes=64)
+        w2_words = const.tile([P, 1, PACK * CODE], U8, align_bytes=64)
+        w2_planes = const.tile([P, 1, CODE], U8, align_bytes=64)
+        nc.vector.memset(w1_planes[:].bitcast(I32), 0)
+        nc.vector.memset(w2_planes[:].bitcast(I32), 0)
+        load_scale_rows(nc, w1_planes, Wq1_scales)
+        load_scale_rows(nc, w2_planes, Wq2_scales)
+        nc.sync.dma_start(
+            out=w1_words[:].bitcast(I32), in_=Wq1_words.rearrange("g p n t -> p g (n t)").bitcast(I32)
+        )
+        nc.sync.dma_start(
+            out=w2_words[:].bitcast(I32), in_=Wq2_words.rearrange("g p n t -> p g (n t)").bitcast(I32)
+        )
+
+        b1_rows = const.tile([P, HIDDEN], BF16)
+        nc.sync.dma_start(out=b1_rows[:], in_=bq1.partition_broadcast(P))
+        b1_by_t = const.tile([P, PACK, P], BF16)
+        nc.vector.tensor_copy(out=b1_by_t[:], in_=b1_rows[:].rearrange("q (p t) -> q t p", t=PACK))
+        b2_rows = const.tile([P, CODE], BF16)
+        nc.sync.dma_start(out=b2_rows[:], in_=bq2.partition_broadcast(P))
+
+        var_by_token = const.tile([P, P], F32)
+        nc.vector.memset(var_by_token[:], 0.0)
+
+        for b in range(1, Z_BUFFERS):
+            load_batch(b)
+
+        x_t, x_sumsq, x_norm, x_inverse, inverse_rows, xn, x_words, x_planes = {}, {}, {}, {}, {}, {}, {}, {}
+        h_sums, h_biased, h_t, h_grouped, h_words, h_planes = {}, {}, {}, {}, {}, {}
+        zq_sums, zq, minus_mean, dev_sumsq, dev_norm = {}, {}, {}, {}, {}
+
+        def invert(norm):
+            floored = small.tile([P, TILES], F32)
+            nc.vector.tensor_scalar_max(out=floored[:], in0=norm[:], scalar1=EPS)
+            inverse = small.tile([P, TILES], F32)
+            nc.vector.reciprocal(out=inverse[:], in_=floored[:])
+            return inverse
+
+        def transpose_tokens(k):
+            b, i = divmod(k, PIXELS // P)
+            x_t[k] = psum_x.tile([P, PASSES * PACK, P], BF16, name="x_t")
+            for g in range(PASSES):
+                for t in range(PACK):
+                    nc.tensor.transpose(
+                        x_t[k][:, g * PACK + t, :], z_sb[b][:, g, t, i * P : (i + 1) * P], ident_bf[:]
+                    )
+
+        def sum_squares(k):
+            c, i = divmod(k, TILES)
+            if i == 0:
+                x_sumsq[c] = small.tile([P, TILES], F32, name="x_sumsq")
+            x_squares = scrap.tile([P, CHANNELS], BF16)
+            nc.scalar.activation(
+                out=x_squares[:],
+                in_=x_t[k][:].rearrange("q a c -> q (a c)"),
+                func=ACT.Square,
+                accum_out=x_sumsq[c][:, i : i + 1],
+            )
+
+        def spread_inverse(c):
+            inverse_rows[c] = psum_r.tile([P, CHUNK], F32, name="inverse_rows")
+            for i in range(TILES):
+                nc.tensor.transpose(
+                    inverse_rows[c][:, i * P : (i + 1) * P],
+                    x_inverse[c][:, i : i + 1].to_broadcast([P, P]),
+                    ident_f32[:],
+                )
+
+        def scale_pass(c, g):
+            b, half = divmod(c, BATCH_CHUNKS)
+            xn[c, g] = stage.tile([P, CHUNK, PACK], BF16, name="xn", align_bytes=64)
+            nc.vector.tensor_tensor(
+                out=xn[c, g][:],
+                in0=z_sb[b][:, g, :, half * CHUNK : (half + 1) * CHUNK].rearrange("p t x -> p x t"),
+                in1=inverse_rows[c][:].unsqueeze(2).to_broadcast([P, CHUNK, PACK]),
+                op=ALU.mult,
+            )
+
+        def quantise_x(c):
+            x_words[c] = packed.tile([P, PASSES, CHUNK], U32, name="x_words", align_bytes=64)
+            x_planes[c] = packed.tile([P, PASSES, CHUNK], U8, name="x_planes", align_bytes=64)
+            for g in range(PASSES):
+                nc.vector.quantize_mx(
+                    out=x_words[c][:, g, :].bitcast(FP8X4),
+                    scales=x_planes[c][:, g, :],
+                    in_=xn[c, g][:].rearrange("p x t -> p (x t)"),
+                )
+
+        def product_1(k):
+            c, i = divmod(k, TILES)
+            h_sums[k] = psum_h.tile([P, HIDDEN], F32, name="h_sums")
+            for g in range(PASSES):
+                nc.tensor.matmul_mx(
+                    out=h_sums[k][:],
+                    lhsT=x_words[c][:, g, i * P : (i + 1) * P].bitcast(FP8X4),
+                    lhsT_scale=x_planes[c][:, g, i * P : (i + 1) * P],
+                    rhs=w1_words[:, g, :].bitcast(FP8X4),
+                    rhs_scale=w1_planes[:, g, :],
+                    start=(g == 0),
+                    stop=(g == PASSES - 1),
+                )
+
+        def add_bias(k):
+            h_biased[k] = stage.tile([P, PACK, P], BF16, name="h_biased")
+            nc.vector.tensor_tensor(
+                out=h_biased[k][:],
+                in0=h_sums[k][:].rearrange("q (p t) -> q t p", t=PACK),
+                in1=b1_by_t[:],
+                op=ALU.add,
+            )
+
+        def transpose_hidden(k):
+            pair, j = divmod(k, 2)
+            if j == 0:
+                h_t[pair] = psum_t.tile([P, 2, PACK, P], BF16, name="h_t")
+            for t in range(PACK):
+                nc.tensor.transpose(h_t[pair][:, j, t, :], h_biased[k][:, t, :], ident_bf[:])
+
+        def relu_pair(pair):
+            c, j = divmod(pair, TILES // 2)
+            if j == 0:
+                h_grouped[c] = stage.tile([P, CHUNK, PACK], BF16, name="h_grouped", align_bytes=64)
+            nc.scalar.activation(
+                out=h_grouped[c][:, 2 * j * P : 2 * (j + 1) * P, :].rearrange("p (j n) t -> p j n t", j=2),
+                in_=h_t[pair][:].rearrange("p j t n -> p j n t"),
+                func=ACT.Relu,
+            )
+
+        def quantise_h(c):
+            h_words[c] = packed.tile([P, CHUNK], U32, name="h_words", align_bytes=64)
+            h_planes[c] = packed.tile([P, CHUNK], U8, name="h_planes", align_bytes=64)
+            nc.vector.quantize_mx(
+                out=h_words[c][:].bitcast(FP8X4),
+                scales=h_planes[c][:],
+                in_=h_grouped[c][:].rearrange("p n t -> p (n t)"),
+            )
+
+        def product_2(c):
+            zq_sums[c] = psum_z.tile([P, TILES, CODE], F32, name="zq_sums")
+            for i in range(TILES):
+                nc.tensor.matmul_mx(
+                    out=zq_sums[c][:, i, :],
+                    lhsT=h_words[c][:, i * P : (i + 1) * P].bitcast(FP8X4),
+                    lhsT_scale=h_planes[c][:, i * P : (i + 1) * P],
+                    rhs=w2_words[:, 0, :].bitcast(FP8X4),
+                    rhs_scale=w2_planes[:, 0, :],
+                    start=True,
+                    stop=True,
+                )
+
+        def centre(c):
+            zq[c] = result.tile([P, TILES, CODE], F32, name="zq")
+            nc.vector.tensor_tensor(
+                out=zq[c][:],
+                in0=zq_sums[c][:],
+                in1=b2_rows[:].unsqueeze(1).to_broadcast([P, TILES, CODE]),
+                op=ALU.add,
+            )
+            zq_total = small.tile([P, TILES], F32)
+            nc.vector.tensor_reduce(out=zq_total[:], in_=zq[c][:], axis=mybir.AxisListType.X, op=ALU.add)
+            minus_mean[c] = small.tile([P, TILES], F32, name="minus_mean")
+            nc.vector.tensor_scalar_mul(out=minus_mean[c][:], in0=zq_total[:], scalar1=-1.0 / CODE)
+
+        def sum_deviations(c):
+            dev_sumsq[c] = small.tile([P, TILES], F32, name="dev_sumsq")
+            for i in range(TILES):
+                dev_squares = scrap.tile([P, CODE], F32)
+                nc.scalar.activation(
+                    out=dev_squares[:],
+                    in_=zq[c][:, i, :],
+                    func=ACT.Square,
+                    bias=minus_mean[c][:, i : i + 1],
+                    accum_out=dev_sumsq[c][:, i : i + 1],
+                )
+
+        def normalise_and_store(c):
+            nc.vector.tensor_scalar_mul(
+                out=var_by_token[:, c * TILES : (c + 1) * TILES], in0=dev_sumsq[c][:], scalar1=1.0 / (CODE - 1)
+            )
+            dev_inverse = invert(dev_norm[c])
+            zc = result.tile([P, TILES, CODE], F32)
+            for i in range(TILES):
+                nc.gpsimd.tensor_scalar(
+                    out=zc[:, i, :],
+                    in0=zq[c][:, i, :],
+                    scalar1=minus_mean[c][:, i : i + 1],
+                    scalar2=dev_inverse[:, i : i + 1],
+                    op0=ALU.add,
+                    op1=ALU.mult,
+                )
+            nc.sync.dma_start(
+                out=out_0[c * CHUNK : (c + 1) * CHUNK, :].rearrange("(i q) d -> q i d", q=P), in_=zc[:]
+            )
+
+        for step in range(STEPS):
+            c = chunk_due(step, CHUNK_SCALE)
+            if c is not None:
+                x_inverse[c] = invert(x_norm[c])
+            k = tile_due(step, TILE_BIAS)
+            if k is not None:
+                add_bias(k)
+
+            if c is not None:
+                spread_inverse(c)
+            k = tile_due(step, 0)
+            if k is not None:
+                transpose_tokens(k)
+            k = tile_due(step, TILE_TRANSPOSE_H)
+            if k is not None:
+                transpose_hidden(k)
+            k = tile_due(step, TILE_PRODUCT_1)
+            if k is not None:
+                product_1(k)
+            c = chunk_due(step, CHUNK_PRODUCT_2)
+            if c is not None:
+                product_2(c)
+
+            k = tile_due(step, TILE_SQUARES)
+            if k is not None:
+                sum_squares(k)
+            c = chunk_due(step, CHUNK_ROOT)
+            if c is not None:
+                x_norm[c] = small.tile([P, TILES], F32, name="x_norm")
+                nc.scalar.sqrt(out=x_norm[c][:], in_=x_sumsq[c][:])
+            k = tile_due(step, TILE_RELU)
+            if k is not None and k % 2 == 1:
+                relu_pair(k // 2)
+            c = chunk_due(step, CHUNK_DEVIATIONS)
+            if c is not None:
+                sum_deviations(c)
+            c = chunk_due(step, CHUNK_DEVIATION_ROOT)
+            if c is not None:
+                dev_norm[c] = small.tile([P, TILES], F32, name="dev_norm")
+                nc.scalar.sqrt(out=dev_norm[c][:], in_=dev_sumsq[c][:])
+
+            for g in range(PASSES):
+                c = chunk_due(step, CHUNK_SCALE + g)
+                if c is not None:
+                    scale_pass(c, g)
+                    last_use_of_batch = g == PASSES - 1 and c % BATCH_CHUNKS == BATCH_CHUNKS - 1
+                    if last_use_of_batch and c // BATCH_CHUNKS + Z_BUFFERS < BATCH:
+                        load_batch(c // BATCH_CHUNKS + Z_BUFFERS)
+            c = chunk_due(step, CHUNK_QUANTISE_X)
+            if c is not None:
+                quantise_x(c)
+            c = chunk_due(step, CHUNK_QUANTISE_H)
+            if c is not None:
+                quantise_h(c)
+            c = chunk_due(step, CHUNK_CENTRE)
+            if c is not None:
+                centre(c)
+            c = chunk_due(step, CHUNK_NORMALISE)
+            if c is not None:
+                normalise_and_store(c)
+
+        var_t = psum_r.tile([P, CHUNK], F32, tag="inverse_rows")
+        nc.tensor.transpose(var_t[:, :P], var_by_token[:], ident_f32[:])
+        var_rows = result.tile([P, P], F32)
+        nc.vector.tensor_copy(out=var_rows[:], in_=var_t[:, :P])
+        nc.sync.dma_start(out=out_1.rearrange("(i q) o -> i (q o)", q=P), in_=var_rows[:TOKEN_TILES, :])

@@ -30,19 +30,19 @@ BATCH_CHUNKS = PIXELS // CHUNK
 Z_BUFFERS = 3
 
 TILE_SQUARES = 1
-CHUNK_ROOT = 2
-CHUNK_SCALE = 3
-CHUNK_QUANTISE_X = 5
-TILE_PRODUCT_1 = 9
-TILE_BIAS = 10
-TILE_TRANSPOSE_H = 11
-TILE_RELU = 12
-CHUNK_QUANTISE_H = 13
-CHUNK_PRODUCT_2 = 15
-CHUNK_CENTRE = 18
-CHUNK_DEVIATIONS = 19
-CHUNK_DEVIATION_ROOT = 20
-CHUNK_NORMALISE = 21
+CHUNK_INVERSE = 2
+CHUNK_SPREAD = 3
+CHUNK_SCALE = 4
+CHUNK_QUANTISE_X = (6, 8)
+TILE_PRODUCT_1 = 12
+TILE_BIAS = 13
+TILE_TRANSPOSE_H = 14
+TILE_RELU = 15
+CHUNK_QUANTISE_H = 17
+CHUNK_PRODUCT_2 = 19
+CHUNK_CENTRE = 22
+CHUNK_DEVIATIONS = 24
+CHUNK_NORMALISE = 25
 STEPS = TOKEN_TILES + CHUNK_NORMALISE
 
 
@@ -120,21 +120,21 @@ def tile_spatialmemorymodule_pb_kernel(
         b2_rows = const.tile([P, CODE], BF16)
         nc.sync.dma_start(out=b2_rows[:], in_=bq2.partition_broadcast(P))
 
-        var_by_token = const.tile([P, P], F32)
-        nc.vector.memset(var_by_token[:], 0.0)
+        dev_sumsq = const.tile([P, P], F32)
+        nc.vector.memset(dev_sumsq[:], 0.0)
 
         for b in range(1, Z_BUFFERS):
             load_batch(b)
 
-        x_t, x_sumsq, x_norm, x_inverse, inverse_rows, xn, x_words, x_planes = {}, {}, {}, {}, {}, {}, {}, {}
+        x_t, x_sumsq, x_inverse, inverse_rows, inverse_copy, xn, x_words, x_planes = {}, {}, {}, {}, {}, {}, {}, {}
         h_sums, h_biased, h_t, h_grouped, h_words, h_planes = {}, {}, {}, {}, {}, {}
-        zq_sums, zq, minus_mean, dev_sumsq, dev_norm = {}, {}, {}, {}, {}
+        zq_sums, zq, minus_mean, dev_inverse = {}, {}, {}, {}
 
-        def invert(norm):
-            floored = small.tile([P, TILES], F32)
-            nc.vector.tensor_scalar_max(out=floored[:], in0=norm[:], scalar1=EPS)
+        def inverse_root(sums, floor):
+            excess = small.tile([P, TILES], F32)
+            nc.scalar.activation(out=excess[:], in_=sums, func=ACT.Relu, bias=-floor)
             inverse = small.tile([P, TILES], F32)
-            nc.vector.reciprocal(out=inverse[:], in_=floored[:])
+            nc.scalar.activation(out=inverse[:], in_=excess[:], func=ACT.Abs_reciprocal_sqrt, bias=floor)
             return inverse
 
         def transpose_tokens(k):
@@ -167,25 +167,25 @@ def tile_spatialmemorymodule_pb_kernel(
                     ident_f32[:],
                 )
 
-        def scale_pass(c, g):
+        def scale_pass(engine, c, g, inverse, first, count):
             b, half = divmod(c, BATCH_CHUNKS)
-            xn[c, g] = stage.tile([P, CHUNK, PACK], BF16, name="xn", align_bytes=64)
-            nc.vector.tensor_tensor(
-                out=xn[c, g][:],
-                in0=z_sb[b][:, g, :, half * CHUNK : (half + 1) * CHUNK].rearrange("p t x -> p x t"),
-                in1=inverse_rows[c][:].unsqueeze(2).to_broadcast([P, CHUNK, PACK]),
+            first_pixel = half * CHUNK + first
+            engine.tensor_tensor(
+                out=xn[c][:, g, first : first + count, :],
+                in0=z_sb[b][:, g, :, first_pixel : first_pixel + count].rearrange("p t x -> p x t"),
+                in1=inverse[:, first : first + count].unsqueeze(2).to_broadcast([P, count, PACK]),
                 op=ALU.mult,
             )
 
-        def quantise_x(c):
-            x_words[c] = packed.tile([P, PASSES, CHUNK], U32, name="x_words", align_bytes=64)
-            x_planes[c] = packed.tile([P, PASSES, CHUNK], U8, name="x_planes", align_bytes=64)
-            for g in range(PASSES):
-                nc.vector.quantize_mx(
-                    out=x_words[c][:, g, :].bitcast(FP8X4),
-                    scales=x_planes[c][:, g, :],
-                    in_=xn[c, g][:].rearrange("p x t -> p (x t)"),
-                )
+        def quantise_x(c, g):
+            if g == 0:
+                x_words[c] = packed.tile([P, PASSES, CHUNK], U32, name="x_words", align_bytes=64)
+                x_planes[c] = packed.tile([P, PASSES, CHUNK], U8, name="x_planes", align_bytes=64)
+            nc.vector.quantize_mx(
+                out=x_words[c][:, g, :].bitcast(FP8X4),
+                scales=x_planes[c][:, g, :],
+                in_=xn[c][:, g].rearrange("p x t -> p (x t)"),
+            )
 
         def product_1(k):
             c, i = divmod(k, TILES)
@@ -263,7 +263,6 @@ def tile_spatialmemorymodule_pb_kernel(
             nc.vector.tensor_scalar_mul(out=minus_mean[c][:], in0=zq_total[:], scalar1=-1.0 / CODE)
 
         def sum_deviations(c):
-            dev_sumsq[c] = small.tile([P, TILES], F32, name="dev_sumsq")
             for i in range(TILES):
                 dev_squares = scrap.tile([P, CODE], F32)
                 nc.scalar.activation(
@@ -271,21 +270,18 @@ def tile_spatialmemorymodule_pb_kernel(
                     in_=zq[c][:, i, :],
                     func=ACT.Square,
                     bias=minus_mean[c][:, i : i + 1],
-                    accum_out=dev_sumsq[c][:, i : i + 1],
+                    accum_out=dev_sumsq[:, c * TILES + i : c * TILES + i + 1],
                 )
+            dev_inverse[c] = inverse_root(dev_sumsq[:, c * TILES : (c + 1) * TILES], EPS * EPS)
 
         def normalise_and_store(c):
-            nc.vector.tensor_scalar_mul(
-                out=var_by_token[:, c * TILES : (c + 1) * TILES], in0=dev_sumsq[c][:], scalar1=1.0 / (CODE - 1)
-            )
-            dev_inverse = invert(dev_norm[c])
             zc = result.tile([P, TILES, CODE], F32)
             for i in range(TILES):
                 nc.gpsimd.tensor_scalar(
                     out=zc[:, i, :],
                     in0=zq[c][:, i, :],
                     scalar1=minus_mean[c][:, i : i + 1],
-                    scalar2=dev_inverse[:, i : i + 1],
+                    scalar2=dev_inverse[c][:, i : i + 1],
                     op0=ALU.add,
                     op1=ALU.mult,
                 )
@@ -294,13 +290,11 @@ def tile_spatialmemorymodule_pb_kernel(
             )
 
         for step in range(STEPS):
-            c = chunk_due(step, CHUNK_SCALE)
-            if c is not None:
-                x_inverse[c] = invert(x_norm[c])
             k = tile_due(step, TILE_BIAS)
             if k is not None:
                 add_bias(k)
 
+            c = chunk_due(step, CHUNK_SPREAD)
             if c is not None:
                 spread_inverse(c)
             k = tile_due(step, 0)
@@ -319,31 +313,35 @@ def tile_spatialmemorymodule_pb_kernel(
             k = tile_due(step, TILE_SQUARES)
             if k is not None:
                 sum_squares(k)
-            c = chunk_due(step, CHUNK_ROOT)
+            c = chunk_due(step, CHUNK_INVERSE)
             if c is not None:
-                x_norm[c] = small.tile([P, TILES], F32, name="x_norm")
-                nc.scalar.sqrt(out=x_norm[c][:], in_=x_sumsq[c][:])
+                x_inverse[c] = inverse_root(x_sumsq[c][:], EPS * EPS)
+            c = chunk_due(step, CHUNK_SCALE)
+            if c is not None:
+                inverse_copy[c] = stage.tile([P, CHUNK], F32, name="inverse_copy")
+                nc.scalar.copy(out=inverse_copy[c][:], in_=inverse_rows[c][:])
             k = tile_due(step, TILE_RELU)
             if k is not None and k % 2 == 1:
                 relu_pair(k // 2)
             c = chunk_due(step, CHUNK_DEVIATIONS)
             if c is not None:
                 sum_deviations(c)
-            c = chunk_due(step, CHUNK_DEVIATION_ROOT)
-            if c is not None:
-                dev_norm[c] = small.tile([P, TILES], F32, name="dev_norm")
-                nc.scalar.sqrt(out=dev_norm[c][:], in_=dev_sumsq[c][:])
 
-            for g in range(PASSES):
-                c = chunk_due(step, CHUNK_SCALE + g)
-                if c is not None:
-                    scale_pass(c, g)
-                    last_use_of_batch = g == PASSES - 1 and c % BATCH_CHUNKS == BATCH_CHUNKS - 1
-                    if last_use_of_batch and c // BATCH_CHUNKS + Z_BUFFERS < BATCH:
-                        load_batch(c // BATCH_CHUNKS + Z_BUFFERS)
-            c = chunk_due(step, CHUNK_QUANTISE_X)
+            c = chunk_due(step, CHUNK_SCALE)
             if c is not None:
-                quantise_x(c)
+                xn[c] = stage.tile([P, PASSES, CHUNK, PACK], BF16, name="xn", align_bytes=64)
+                scale_pass(nc.vector, c, 0, inverse_rows[c], 0, CHUNK // 2)
+                scale_pass(nc.gpsimd, c, 1, inverse_copy[c], 0, CHUNK)
+            c = chunk_due(step, CHUNK_SCALE + 1)
+            if c is not None:
+                scale_pass(nc.vector, c, 0, inverse_rows[c], CHUNK // 2, CHUNK // 2)
+                last_use_of_batch = c % BATCH_CHUNKS == BATCH_CHUNKS - 1
+                if last_use_of_batch and c // BATCH_CHUNKS + Z_BUFFERS < BATCH:
+                    load_batch(c // BATCH_CHUNKS + Z_BUFFERS)
+            for g in range(PASSES):
+                c = chunk_due(step, CHUNK_QUANTISE_X[g])
+                if c is not None:
+                    quantise_x(c, g)
             c = chunk_due(step, CHUNK_QUANTISE_H)
             if c is not None:
                 quantise_h(c)
@@ -355,7 +353,7 @@ def tile_spatialmemorymodule_pb_kernel(
                 normalise_and_store(c)
 
         var_t = psum_r.tile([P, CHUNK], F32, tag="inverse_rows")
-        nc.tensor.transpose(var_t[:, :P], var_by_token[:], ident_f32[:])
+        nc.tensor.transpose(var_t[:, :P], dev_sumsq[:], ident_f32[:])
         var_rows = result.tile([P, P], F32)
-        nc.vector.tensor_copy(out=var_rows[:], in_=var_t[:, :P])
+        nc.vector.tensor_scalar_mul(out=var_rows[:], in0=var_t[:, :P], scalar1=1.0 / (CODE - 1))
         nc.sync.dma_start(out=out_1.rearrange("(i q) o -> i (q o)", q=P), in_=var_rows[:TOKEN_TILES, :])

@@ -32,17 +32,19 @@ Z_BUFFERS = 3
 TILE_SQUARES = 1
 CHUNK_INVERSE = 2
 CHUNK_SPREAD = 3
-CHUNK_SCALE = 4
-CHUNK_QUANTISE_X = (6, 8)
-TILE_PRODUCT_1 = 12
-TILE_BIAS = 13
-TILE_TRANSPOSE_H = 14
-TILE_RELU = 15
-CHUNK_QUANTISE_H = 17
+CHUNK_COPY_INVERSE = 4
+CHUNK_SCALE = 5
+CHUNK_QUANTISE_X = (7, 9)
+TILE_PRODUCT_1 = 13
+TILE_BIAS = 14
+TILE_TRANSPOSE_H = 15
+TILE_RELU = 16
+CHUNK_QUANTISE_H = 18
 CHUNK_PRODUCT_2 = 19
-CHUNK_CENTRE = 22
-CHUNK_DEVIATIONS = 24
-CHUNK_NORMALISE = 25
+CHUNK_CENTRE = 20
+CHUNK_DEVIATIONS = 21
+CHUNK_SHIFT = 22
+CHUNK_NORMALISE = 23
 STEPS = TOKEN_TILES + CHUNK_NORMALISE
 
 
@@ -128,7 +130,7 @@ def tile_spatialmemorymodule_pb_kernel(
 
         x_t, x_sumsq, x_inverse, inverse_rows, inverse_copy, xn, x_words, x_planes = {}, {}, {}, {}, {}, {}, {}, {}
         h_sums, h_biased, h_t, h_grouped, h_words, h_planes = {}, {}, {}, {}, {}, {}
-        zq_sums, zq, minus_mean, dev_inverse = {}, {}, {}, {}
+        zq_sums, zq, minus_mean, dev_inverse, shift = {}, {}, {}, {}, {}
 
         def inverse_root(sums, floor):
             excess = small.tile([P, TILES], F32)
@@ -167,13 +169,18 @@ def tile_spatialmemorymodule_pb_kernel(
                     ident_f32[:],
                 )
 
-        def scale_pass(engine, c, g, inverse, first, count):
+        def scale_piece(c, piece):
+            g, side = divmod(piece, 2)
             b, half = divmod(c, BATCH_CHUNKS)
+            if piece == 0:
+                xn[c] = stage.tile([P, PASSES, CHUNK, PACK], BF16, name="xn", align_bytes=64)
+            count = CHUNK // 2
+            first = side * count
             first_pixel = half * CHUNK + first
-            engine.tensor_tensor(
+            nc.vector.tensor_tensor(
                 out=xn[c][:, g, first : first + count, :],
                 in0=z_sb[b][:, g, :, first_pixel : first_pixel + count].rearrange("p t x -> p x t"),
-                in1=inverse[:, first : first + count].unsqueeze(2).to_broadcast([P, count, PACK]),
+                in1=inverse_copy[c][:, first : first + count].unsqueeze(2).to_broadcast([P, count, PACK]),
                 op=ALU.mult,
             )
 
@@ -277,13 +284,12 @@ def tile_spatialmemorymodule_pb_kernel(
         def normalise_and_store(c):
             zc = result.tile([P, TILES, CODE], F32)
             for i in range(TILES):
-                nc.gpsimd.tensor_scalar(
+                nc.scalar.activation(
                     out=zc[:, i, :],
-                    in0=zq[c][:, i, :],
-                    scalar1=minus_mean[c][:, i : i + 1],
-                    scalar2=dev_inverse[c][:, i : i + 1],
-                    op0=ALU.add,
-                    op1=ALU.mult,
+                    in_=zq[c][:, i, :],
+                    func=ACT.Identity,
+                    scale=dev_inverse[c][:, i : i + 1],
+                    bias=shift[c][:, i : i + 1],
                 )
             nc.sync.dma_start(
                 out=out_0[c * CHUNK : (c + 1) * CHUNK, :].rearrange("(i q) d -> q i d", q=P), in_=zc[:]
@@ -316,7 +322,7 @@ def tile_spatialmemorymodule_pb_kernel(
             c = chunk_due(step, CHUNK_INVERSE)
             if c is not None:
                 x_inverse[c] = inverse_root(x_sumsq[c][:], EPS * EPS)
-            c = chunk_due(step, CHUNK_SCALE)
+            c = chunk_due(step, CHUNK_COPY_INVERSE)
             if c is not None:
                 inverse_copy[c] = stage.tile([P, CHUNK], F32, name="inverse_copy")
                 nc.scalar.copy(out=inverse_copy[c][:], in_=inverse_rows[c][:])
@@ -327,17 +333,17 @@ def tile_spatialmemorymodule_pb_kernel(
             if c is not None:
                 sum_deviations(c)
 
-            c = chunk_due(step, CHUNK_SCALE)
+            c = chunk_due(step, CHUNK_NORMALISE)
             if c is not None:
-                xn[c] = stage.tile([P, PASSES, CHUNK, PACK], BF16, name="xn", align_bytes=64)
-                scale_pass(nc.vector, c, 0, inverse_rows[c], 0, CHUNK // 2)
-                scale_pass(nc.gpsimd, c, 1, inverse_copy[c], 0, CHUNK)
-            c = chunk_due(step, CHUNK_SCALE + 1)
-            if c is not None:
-                scale_pass(nc.vector, c, 0, inverse_rows[c], CHUNK // 2, CHUNK // 2)
-                last_use_of_batch = c % BATCH_CHUNKS == BATCH_CHUNKS - 1
-                if last_use_of_batch and c // BATCH_CHUNKS + Z_BUFFERS < BATCH:
-                    load_batch(c // BATCH_CHUNKS + Z_BUFFERS)
+                normalise_and_store(c)
+
+            for piece in range(2 * PASSES):
+                c = chunk_due(step, CHUNK_SCALE + piece)
+                if c is not None:
+                    scale_piece(c, piece)
+                    last_use_of_batch = piece == 2 * PASSES - 1 and c % BATCH_CHUNKS == BATCH_CHUNKS - 1
+                    if last_use_of_batch and c // BATCH_CHUNKS + Z_BUFFERS < BATCH:
+                        load_batch(c // BATCH_CHUNKS + Z_BUFFERS)
             for g in range(PASSES):
                 c = chunk_due(step, CHUNK_QUANTISE_X[g])
                 if c is not None:
@@ -348,9 +354,10 @@ def tile_spatialmemorymodule_pb_kernel(
             c = chunk_due(step, CHUNK_CENTRE)
             if c is not None:
                 centre(c)
-            c = chunk_due(step, CHUNK_NORMALISE)
+            c = chunk_due(step, CHUNK_SHIFT)
             if c is not None:
-                normalise_and_store(c)
+                shift[c] = small.tile([P, TILES], F32, name="shift")
+                nc.vector.tensor_tensor(out=shift[c][:], in0=minus_mean[c][:], in1=dev_inverse[c][:], op=ALU.mult)
 
         var_t = psum_r.tile([P, CHUNK], F32, tag="inverse_rows")
         nc.tensor.transpose(var_t[:, :P], dev_sumsq[:], ident_f32[:])

@@ -34,17 +34,17 @@ CHUNK_INVERSE = 2
 CHUNK_SPREAD = 3
 CHUNK_COPY_INVERSE = 4
 CHUNK_SCALE = 5
-CHUNK_QUANTISE_X = (7, 9)
-TILE_PRODUCT_1 = 13
-TILE_BIAS = 14
-TILE_TRANSPOSE_H = 15
-TILE_RELU = 16
-CHUNK_QUANTISE_H = 18
-CHUNK_PRODUCT_2 = 19
-CHUNK_CENTRE = 20
-CHUNK_DEVIATIONS = 21
-CHUNK_SHIFT = 22
-CHUNK_NORMALISE = 23
+CHUNK_QUANTISE_X = 8
+TILE_PRODUCT_1 = 12
+TILE_BIAS = 13
+TILE_TRANSPOSE_H = 14
+TILE_RELU = 15
+CHUNK_QUANTISE_H = 16
+CHUNK_PRODUCT_2 = 17
+CHUNK_CENTRE = 19
+CHUNK_DEVIATIONS = 20
+CHUNK_SHIFT = 21
+CHUNK_NORMALISE = 22
 STEPS = TOKEN_TILES + CHUNK_NORMALISE
 
 
@@ -169,29 +169,23 @@ def tile_spatialmemorymodule_pb_kernel(
                     ident_f32[:],
                 )
 
-        def scale_piece(c, piece):
-            g, side = divmod(piece, 2)
+        def scale_pass(engine, c, g, inverse, first, count):
             b, half = divmod(c, BATCH_CHUNKS)
-            if piece == 0:
-                xn[c] = stage.tile([P, PASSES, CHUNK, PACK], BF16, name="xn", align_bytes=64)
-            count = CHUNK // 2
-            first = side * count
             first_pixel = half * CHUNK + first
-            nc.vector.tensor_tensor(
+            engine.tensor_tensor(
                 out=xn[c][:, g, first : first + count, :],
                 in0=z_sb[b][:, g, :, first_pixel : first_pixel + count].rearrange("p t x -> p x t"),
-                in1=inverse_copy[c][:, first : first + count].unsqueeze(2).to_broadcast([P, count, PACK]),
+                in1=inverse[:, first : first + count].unsqueeze(2).to_broadcast([P, count, PACK]),
                 op=ALU.mult,
             )
 
-        def quantise_x(c, g):
-            if g == 0:
-                x_words[c] = packed.tile([P, PASSES, CHUNK], U32, name="x_words", align_bytes=64)
-                x_planes[c] = packed.tile([P, PASSES, CHUNK], U8, name="x_planes", align_bytes=64)
+        def quantise_x(c):
+            x_words[c] = packed.tile([P, PASSES, CHUNK], U32, name="x_words", align_bytes=64)
+            x_planes[c] = packed.tile([P, PASSES, CHUNK], U8, name="x_planes", align_bytes=64)
             nc.vector.quantize_mx(
-                out=x_words[c][:, g, :].bitcast(FP8X4),
-                scales=x_planes[c][:, g, :],
-                in_=xn[c][:, g].rearrange("p x t -> p (x t)"),
+                out=x_words[c][:].rearrange("p g x -> p (g x)").bitcast(FP8X4),
+                scales=x_planes[c][:].rearrange("p g x -> p (g x)"),
+                in_=xn[c][:].rearrange("p g x t -> p (g x t)"),
             )
 
         def product_1(k):
@@ -322,10 +316,6 @@ def tile_spatialmemorymodule_pb_kernel(
             c = chunk_due(step, CHUNK_INVERSE)
             if c is not None:
                 x_inverse[c] = inverse_root(x_sumsq[c][:], EPS * EPS)
-            c = chunk_due(step, CHUNK_COPY_INVERSE)
-            if c is not None:
-                inverse_copy[c] = stage.tile([P, CHUNK], F32, name="inverse_copy")
-                nc.scalar.copy(out=inverse_copy[c][:], in_=inverse_rows[c][:])
             k = tile_due(step, TILE_RELU)
             if k is not None and k % 2 == 1:
                 relu_pair(k // 2)
@@ -337,20 +327,25 @@ def tile_spatialmemorymodule_pb_kernel(
             if c is not None:
                 normalise_and_store(c)
 
-            for piece in range(2 * PASSES):
-                c = chunk_due(step, CHUNK_SCALE + piece)
-                if c is not None:
-                    scale_piece(c, piece)
-                    last_use_of_batch = piece == 2 * PASSES - 1 and c % BATCH_CHUNKS == BATCH_CHUNKS - 1
-                    if last_use_of_batch and c // BATCH_CHUNKS + Z_BUFFERS < BATCH:
-                        load_batch(c // BATCH_CHUNKS + Z_BUFFERS)
-            for g in range(PASSES):
-                c = chunk_due(step, CHUNK_QUANTISE_X[g])
-                if c is not None:
-                    quantise_x(c, g)
+            c = chunk_due(step, CHUNK_QUANTISE_X)
+            if c is not None:
+                quantise_x(c)
             c = chunk_due(step, CHUNK_QUANTISE_H)
             if c is not None:
                 quantise_h(c)
+            c = chunk_due(step, CHUNK_COPY_INVERSE)
+            if c is not None:
+                inverse_copy[c] = stage.tile([P, CHUNK], F32, name="inverse_copy")
+                nc.vector.tensor_copy(out=inverse_copy[c][:], in_=inverse_rows[c][:])
+                xn[c] = stage.tile([P, PASSES, CHUNK, PACK], BF16, name="xn", align_bytes=64)
+                scale_pass(nc.gpsimd, c, 1, inverse_copy[c], 0, CHUNK)
+            for side in range(2):
+                c = chunk_due(step, CHUNK_SCALE + side)
+                if c is not None:
+                    scale_pass(nc.vector, c, 0, inverse_rows[c], side * (CHUNK // 2), CHUNK // 2)
+                    last_use_of_batch = side == 1 and c % BATCH_CHUNKS == BATCH_CHUNKS - 1
+                    if last_use_of_batch and c // BATCH_CHUNKS + Z_BUFFERS < BATCH:
+                        load_batch(c // BATCH_CHUNKS + Z_BUFFERS)
             c = chunk_due(step, CHUNK_CENTRE)
             if c is not None:
                 centre(c)

@@ -27,24 +27,24 @@ FLOPS = 2 * BATCH * PIXELS * (CHANNELS * HIDDEN + HIDDEN * CODE)
 
 TOKEN_TILES = BATCH * PIXELS // P
 BATCH_CHUNKS = PIXELS // CHUNK
-Z_BUFFERS = 3
+Z_BUFFERS = 6
 
 TILE_SQUARES = 1
 CHUNK_INVERSE = 2
 CHUNK_SPREAD = 3
 CHUNK_COPY_INVERSE = 4
 CHUNK_SCALE = 5
-CHUNK_QUANTISE_X = 8
-TILE_PRODUCT_1 = 12
-TILE_BIAS = 13
-TILE_TRANSPOSE_H = 14
-TILE_RELU = 15
-CHUNK_QUANTISE_H = 16
-CHUNK_PRODUCT_2 = 17
-CHUNK_CENTRE = 19
-CHUNK_DEVIATIONS = 20
-CHUNK_SHIFT = 21
-CHUNK_NORMALISE = 22
+CHUNK_QUANTISE_X = (7, 9)
+TILE_PRODUCT_1 = 13
+TILE_BIAS = 14
+TILE_TRANSPOSE_H = 15
+TILE_RELU = 16
+CHUNK_QUANTISE_H = 18
+CHUNK_PRODUCT_2 = 19
+CHUNK_BIAS_2 = 20
+CHUNK_MEAN = 21
+CHUNK_DEVIATIONS = 23
+CHUNK_NORMALISE = 24
 STEPS = TOKEN_TILES + CHUNK_NORMALISE
 
 
@@ -87,13 +87,14 @@ def tile_spatialmemorymodule_pb_kernel(
 
         z_sb = {}
 
-        def load_batch(b):
-            z_sb[b] = z_pool.tile([P, PASSES, PACK, PIXELS], BF16, name="z_sb")
+        def load_chunk(c):
+            b, half = divmod(c, BATCH_CHUNKS)
+            z_sb[c] = z_pool.tile([P, PASSES, PACK, CHUNK], BF16, name="z_sb")
             for g in range(PASSES):
-                rows = z[b, g * P * PACK : (g + 1) * P * PACK]
-                nc.sync.dma_start(out=z_sb[b][:, g], in_=rows.rearrange("(p t) h w -> p t (h w)", t=PACK))
+                rows = z[b, g * P * PACK : (g + 1) * P * PACK].rearrange("(p t) h w -> p t (h w)", t=PACK)
+                nc.sync.dma_start(out=z_sb[c][:, g], in_=rows[:, :, half * CHUNK : (half + 1) * CHUNK])
 
-        load_batch(0)
+        load_chunk(0)
 
         ident_bf = const.tile([P, P], BF16)
         make_identity(nc, ident_bf[:])
@@ -125,12 +126,12 @@ def tile_spatialmemorymodule_pb_kernel(
         dev_sumsq = const.tile([P, P], F32)
         nc.vector.memset(dev_sumsq[:], 0.0)
 
-        for b in range(1, Z_BUFFERS):
-            load_batch(b)
+        for c in range(1, Z_BUFFERS):
+            load_chunk(c)
 
         x_t, x_sumsq, x_inverse, inverse_rows, inverse_copy, xn, x_words, x_planes = {}, {}, {}, {}, {}, {}, {}, {}
         h_sums, h_biased, h_t, h_grouped, h_words, h_planes = {}, {}, {}, {}, {}, {}
-        zq_sums, zq, minus_mean, dev_inverse, shift = {}, {}, {}, {}, {}
+        zq_sums, zq, minus_mean, dev_inverse = {}, {}, {}, {}
 
         def inverse_root(sums, floor):
             excess = small.tile([P, TILES], F32)
@@ -140,12 +141,12 @@ def tile_spatialmemorymodule_pb_kernel(
             return inverse
 
         def transpose_tokens(k):
-            b, i = divmod(k, PIXELS // P)
+            c, i = divmod(k, TILES)
             x_t[k] = psum_x.tile([P, PASSES * PACK, P], BF16, name="x_t")
             for g in range(PASSES):
                 for t in range(PACK):
                     nc.tensor.transpose(
-                        x_t[k][:, g * PACK + t, :], z_sb[b][:, g, t, i * P : (i + 1) * P], ident_bf[:]
+                        x_t[k][:, g * PACK + t, :], z_sb[c][:, g, t, i * P : (i + 1) * P], ident_bf[:]
                     )
 
         def sum_squares(k):
@@ -169,23 +170,27 @@ def tile_spatialmemorymodule_pb_kernel(
                     ident_f32[:],
                 )
 
-        def scale_pass(engine, c, g, inverse, first, count):
-            b, half = divmod(c, BATCH_CHUNKS)
-            first_pixel = half * CHUNK + first
-            engine.tensor_tensor(
+        def scale_piece(c, piece):
+            g, side = divmod(piece, 2)
+            if piece == 0:
+                xn[c] = stage.tile([P, PASSES, CHUNK, PACK], BF16, name="xn", align_bytes=64)
+            count = CHUNK // 2
+            first = side * count
+            nc.vector.tensor_tensor(
                 out=xn[c][:, g, first : first + count, :],
-                in0=z_sb[b][:, g, :, first_pixel : first_pixel + count].rearrange("p t x -> p x t"),
-                in1=inverse[:, first : first + count].unsqueeze(2).to_broadcast([P, count, PACK]),
+                in0=z_sb[c][:, g, :, first : first + count].rearrange("p t x -> p x t"),
+                in1=inverse_copy[c][:, first : first + count].unsqueeze(2).to_broadcast([P, count, PACK]),
                 op=ALU.mult,
             )
 
-        def quantise_x(c):
-            x_words[c] = packed.tile([P, PASSES, CHUNK], U32, name="x_words", align_bytes=64)
-            x_planes[c] = packed.tile([P, PASSES, CHUNK], U8, name="x_planes", align_bytes=64)
+        def quantise_x(c, g):
+            if g == 0:
+                x_words[c] = packed.tile([P, PASSES, CHUNK], U32, name="x_words", align_bytes=64)
+                x_planes[c] = packed.tile([P, PASSES, CHUNK], U8, name="x_planes", align_bytes=64)
             nc.vector.quantize_mx(
-                out=x_words[c][:].rearrange("p g x -> p (g x)").bitcast(FP8X4),
-                scales=x_planes[c][:].rearrange("p g x -> p (g x)"),
-                in_=xn[c][:].rearrange("p g x t -> p (g x t)"),
+                out=x_words[c][:, g, :].bitcast(FP8X4),
+                scales=x_planes[c][:, g, :],
+                in_=xn[c][:, g].rearrange("p x t -> p (x t)"),
             )
 
         def product_1(k):
@@ -250,7 +255,7 @@ def tile_spatialmemorymodule_pb_kernel(
                     stop=True,
                 )
 
-        def centre(c):
+        def add_bias_2(c):
             zq[c] = result.tile([P, TILES, CODE], F32, name="zq")
             nc.vector.tensor_tensor(
                 out=zq[c][:],
@@ -258,10 +263,18 @@ def tile_spatialmemorymodule_pb_kernel(
                 in1=b2_rows[:].unsqueeze(1).to_broadcast([P, TILES, CODE]),
                 op=ALU.add,
             )
-            zq_total = small.tile([P, TILES], F32)
-            nc.vector.tensor_reduce(out=zq_total[:], in_=zq[c][:], axis=mybir.AxisListType.X, op=ALU.add)
+
+        def mean(c):
             minus_mean[c] = small.tile([P, TILES], F32, name="minus_mean")
-            nc.vector.tensor_scalar_mul(out=minus_mean[c][:], in0=zq_total[:], scalar1=-1.0 / CODE)
+            for i in range(TILES):
+                shares = scrap.tile([P, CODE], F32)
+                nc.scalar.activation(
+                    out=shares[:],
+                    in_=zq[c][:, i, :],
+                    func=ACT.Identity,
+                    scale=-1.0 / CODE,
+                    accum_out=minus_mean[c][:, i : i + 1],
+                )
 
         def sum_deviations(c):
             for i in range(TILES):
@@ -278,12 +291,13 @@ def tile_spatialmemorymodule_pb_kernel(
         def normalise_and_store(c):
             zc = result.tile([P, TILES, CODE], F32)
             for i in range(TILES):
-                nc.scalar.activation(
+                nc.gpsimd.tensor_scalar(
                     out=zc[:, i, :],
-                    in_=zq[c][:, i, :],
-                    func=ACT.Identity,
-                    scale=dev_inverse[c][:, i : i + 1],
-                    bias=shift[c][:, i : i + 1],
+                    in0=zq[c][:, i, :],
+                    scalar1=minus_mean[c][:, i : i + 1],
+                    scalar2=dev_inverse[c][:, i : i + 1],
+                    op0=ALU.add,
+                    op1=ALU.mult,
                 )
             nc.sync.dma_start(
                 out=out_0[c * CHUNK : (c + 1) * CHUNK, :].rearrange("(i q) d -> q i d", q=P), in_=zc[:]
@@ -316,43 +330,40 @@ def tile_spatialmemorymodule_pb_kernel(
             c = chunk_due(step, CHUNK_INVERSE)
             if c is not None:
                 x_inverse[c] = inverse_root(x_sumsq[c][:], EPS * EPS)
+            c = chunk_due(step, CHUNK_COPY_INVERSE)
+            if c is not None:
+                inverse_copy[c] = stage.tile([P, CHUNK], F32, name="inverse_copy")
+                nc.scalar.copy(out=inverse_copy[c][:], in_=inverse_rows[c][:])
             k = tile_due(step, TILE_RELU)
             if k is not None and k % 2 == 1:
                 relu_pair(k // 2)
+            c = chunk_due(step, CHUNK_MEAN)
+            if c is not None:
+                mean(c)
             c = chunk_due(step, CHUNK_DEVIATIONS)
             if c is not None:
                 sum_deviations(c)
 
-            c = chunk_due(step, CHUNK_NORMALISE)
-            if c is not None:
-                normalise_and_store(c)
-
-            c = chunk_due(step, CHUNK_QUANTISE_X)
-            if c is not None:
-                quantise_x(c)
+            for piece in range(2 * PASSES):
+                c = chunk_due(step, CHUNK_SCALE + piece)
+                if c is not None:
+                    scale_piece(c, piece)
+                    if piece == 2 * PASSES - 1 and c + Z_BUFFERS < CHUNKS:
+                        load_chunk(c + Z_BUFFERS)
+            for g in range(PASSES):
+                c = chunk_due(step, CHUNK_QUANTISE_X[g])
+                if c is not None:
+                    quantise_x(c, g)
             c = chunk_due(step, CHUNK_QUANTISE_H)
             if c is not None:
                 quantise_h(c)
-            c = chunk_due(step, CHUNK_COPY_INVERSE)
+            c = chunk_due(step, CHUNK_BIAS_2)
             if c is not None:
-                inverse_copy[c] = stage.tile([P, CHUNK], F32, name="inverse_copy")
-                nc.vector.tensor_copy(out=inverse_copy[c][:], in_=inverse_rows[c][:])
-                xn[c] = stage.tile([P, PASSES, CHUNK, PACK], BF16, name="xn", align_bytes=64)
-                scale_pass(nc.gpsimd, c, 1, inverse_copy[c], 0, CHUNK)
-            for side in range(2):
-                c = chunk_due(step, CHUNK_SCALE + side)
-                if c is not None:
-                    scale_pass(nc.vector, c, 0, inverse_rows[c], side * (CHUNK // 2), CHUNK // 2)
-                    last_use_of_batch = side == 1 and c % BATCH_CHUNKS == BATCH_CHUNKS - 1
-                    if last_use_of_batch and c // BATCH_CHUNKS + Z_BUFFERS < BATCH:
-                        load_batch(c // BATCH_CHUNKS + Z_BUFFERS)
-            c = chunk_due(step, CHUNK_CENTRE)
+                add_bias_2(c)
+
+            c = chunk_due(step, CHUNK_NORMALISE)
             if c is not None:
-                centre(c)
-            c = chunk_due(step, CHUNK_SHIFT)
-            if c is not None:
-                shift[c] = small.tile([P, TILES], F32, name="shift")
-                nc.vector.tensor_tensor(out=shift[c][:], in0=minus_mean[c][:], in1=dev_inverse[c][:], op=ALU.mult)
+                normalise_and_store(c)
 
         var_t = psum_r.tile([P, CHUNK], F32, tag="inverse_rows")
         nc.tensor.transpose(var_t[:, :P], dev_sumsq[:], ident_f32[:])

@@ -308,21 +308,24 @@ def tile_spatialmemorymodule_pb_kernel(
             if k is not None:
                 add_bias(k)
 
-            c = chunk_due(step, CHUNK_SPREAD)
-            if c is not None:
-                spread_inverse(c)
-            k = tile_due(step, 0)
-            if k is not None:
-                transpose_tokens(k)
-            k = tile_due(step, TILE_TRANSPOSE_H)
-            if k is not None:
-                transpose_hidden(k)
-            k = tile_due(step, TILE_PRODUCT_1)
-            if k is not None:
-                product_1(k)
-            c = chunk_due(step, CHUNK_PRODUCT_2)
-            if c is not None:
-                product_2(c)
+            for kind in ("transposes", "products") if step % 2 == 0 else ("products", "transposes"):
+                if kind == "transposes":
+                    c = chunk_due(step, CHUNK_SPREAD)
+                    if c is not None:
+                        spread_inverse(c)
+                    k = tile_due(step, 0)
+                    if k is not None:
+                        transpose_tokens(k)
+                    k = tile_due(step, TILE_TRANSPOSE_H)
+                    if k is not None:
+                        transpose_hidden(k)
+                else:
+                    k = tile_due(step, TILE_PRODUCT_1)
+                    if k is not None:
+                        product_1(k)
+                    c = chunk_due(step, CHUNK_PRODUCT_2)
+                    if c is not None:
+                        product_2(c)
 
             k = tile_due(step, TILE_SQUARES)
             if k is not None:

@@ -29,22 +29,22 @@ TOKEN_TILES = BATCH * PIXELS // P
 BATCH_CHUNKS = PIXELS // CHUNK
 Z_BUFFERS = 6
 
-TILE_SQUARES = 1
-CHUNK_INVERSE = 2
-CHUNK_SPREAD = 3
-CHUNK_COPY_INVERSE = 4
-CHUNK_SCALE = 5
-CHUNK_QUANTISE_X = (7, 9)
-TILE_PRODUCT_1 = 13
-TILE_BIAS = 14
-TILE_TRANSPOSE_H = 15
-TILE_RELU = 16
-CHUNK_QUANTISE_H = 18
-CHUNK_PRODUCT_2 = 19
-CHUNK_BIAS_2 = 20
-CHUNK_MEAN = 21
-CHUNK_DEVIATIONS = 23
-CHUNK_NORMALISE = 24
+TILE_SQUARES = 2
+CHUNK_INVERSE = 3
+CHUNK_SPREAD = 4
+CHUNK_COPY_INVERSE = 5
+CHUNK_SCALE = 6
+CHUNK_QUANTISE_X = (8, 10)
+TILE_PRODUCT_1 = 14
+TILE_BIAS = 15
+TILE_TRANSPOSE_H = 16
+TILE_RELU = 17
+CHUNK_QUANTISE_H = 21
+CHUNK_PRODUCT_2 = 22
+CHUNK_BIAS_2 = 23
+CHUNK_MEAN = 24
+CHUNK_DEVIATIONS = 26
+CHUNK_NORMALISE = 27
 STEPS = TOKEN_TILES + CHUNK_NORMALISE
 
 
@@ -79,11 +79,10 @@ def tile_spatialmemorymodule_pb_kernel(
         stage = stack.enter_context(tc.tile_pool(name="stage", bufs=4))
         packed = stack.enter_context(tc.tile_pool(name="packed", bufs=3))
         result = stack.enter_context(tc.tile_pool(name="result", bufs=3))
-        psum_x = stack.enter_context(tc.psum_pool(name="psum_x", bufs=2))
+        psum_x = stack.enter_context(tc.psum_pool(name="psum_x", bufs=3))
         psum_r = stack.enter_context(tc.psum_pool(name="psum_r", bufs=1))
         psum_h = stack.enter_context(tc.psum_pool(name="psum_h", bufs=2))
         psum_t = stack.enter_context(tc.psum_pool(name="psum_t", bufs=2))
-        psum_z = stack.enter_context(tc.psum_pool(name="psum_z", bufs=1))
 
         z_sb = {}
 
@@ -162,7 +161,7 @@ def tile_spatialmemorymodule_pb_kernel(
             )
 
         def spread_inverse(c):
-            inverse_rows[c] = psum_r.tile([P, CHUNK], F32, name="inverse_rows")
+            inverse_rows[c] = psum_r.tile([P, CHUNK], F32, name="inverse_rows", tag="shared")
             for i in range(TILES):
                 nc.tensor.transpose(
                     inverse_rows[c][:, i * P : (i + 1) * P],
@@ -243,7 +242,7 @@ def tile_spatialmemorymodule_pb_kernel(
             )
 
         def product_2(c):
-            zq_sums[c] = psum_z.tile([P, TILES, CODE], F32, name="zq_sums")
+            zq_sums[c] = psum_r.tile([P, TILES, CODE], F32, name="zq_sums", tag="shared")
             for i in range(TILES):
                 nc.tensor.matmul_mx(
                     out=zq_sums[c][:, i, :],
@@ -307,25 +306,25 @@ def tile_spatialmemorymodule_pb_kernel(
             k = tile_due(step, TILE_BIAS)
             if k is not None:
                 add_bias(k)
+            c = chunk_due(step, CHUNK_BIAS_2)
+            if c is not None:
+                add_bias_2(c)
 
-            for kind in ("transposes", "products") if step % 2 == 0 else ("products", "transposes"):
-                if kind == "transposes":
-                    c = chunk_due(step, CHUNK_SPREAD)
-                    if c is not None:
-                        spread_inverse(c)
-                    k = tile_due(step, 0)
-                    if k is not None:
-                        transpose_tokens(k)
-                    k = tile_due(step, TILE_TRANSPOSE_H)
-                    if k is not None:
-                        transpose_hidden(k)
-                else:
-                    k = tile_due(step, TILE_PRODUCT_1)
-                    if k is not None:
-                        product_1(k)
-                    c = chunk_due(step, CHUNK_PRODUCT_2)
-                    if c is not None:
-                        product_2(c)
+            k = tile_due(step, 0)
+            if k is not None:
+                transpose_tokens(k)
+            k = tile_due(step, TILE_TRANSPOSE_H)
+            if k is not None:
+                transpose_hidden(k)
+            c = chunk_due(step, CHUNK_SPREAD)
+            if c is not None:
+                spread_inverse(c)
+            k = tile_due(step, TILE_PRODUCT_1)
+            if k is not None:
+                product_1(k)
+            c = chunk_due(step, CHUNK_PRODUCT_2)
+            if c is not None:
+                product_2(c)
 
             k = tile_due(step, TILE_SQUARES)
             if k is not None:
@@ -360,15 +359,12 @@ def tile_spatialmemorymodule_pb_kernel(
             c = chunk_due(step, CHUNK_QUANTISE_H)
             if c is not None:
                 quantise_h(c)
-            c = chunk_due(step, CHUNK_BIAS_2)
-            if c is not None:
-                add_bias_2(c)
 
             c = chunk_due(step, CHUNK_NORMALISE)
             if c is not None:
                 normalise_and_store(c)
 
-        var_t = psum_r.tile([P, CHUNK], F32, tag="inverse_rows")
+        var_t = psum_r.tile([P, CHUNK], F32, tag="shared")
         nc.tensor.transpose(var_t[:, :P], dev_sumsq[:], ident_f32[:])
         var_rows = result.tile([P, P], F32)
         nc.vector.tensor_scalar_mul(out=var_rows[:], in0=var_t[:, :P], scalar1=1.0 / (CODE - 1))

@@ -30,21 +30,19 @@ BATCH_CHUNKS = PIXELS // CHUNK
 Z_BUFFERS = 6
 
 TILE_SQUARES = 2
-CHUNK_INVERSE = 3
-CHUNK_SPREAD = 4
-CHUNK_COPY_INVERSE = 5
-CHUNK_SCALE = 6
-CHUNK_QUANTISE_X = (8, 10)
-TILE_PRODUCT_1 = 14
-TILE_BIAS = 15
-TILE_TRANSPOSE_H = 16
-TILE_RELU = 17
-CHUNK_QUANTISE_H = 21
-CHUNK_PRODUCT_2 = 22
-CHUNK_BIAS_2 = 23
-CHUNK_MEAN = 24
-CHUNK_DEVIATIONS = 26
-CHUNK_NORMALISE = 27
+CHUNK_INVERSE = 2
+CHUNK_SPREAD = 3
+CHUNK_SCALE = 5
+CHUNK_QUANTISE_X = (7, 9)
+CHUNK_PRODUCT_1 = 10
+CHUNK_RELU = 11
+CHUNK_GROUP_H = 15
+CHUNK_QUANTISE_H = 20
+CHUNK_PRODUCT_2 = 21
+CHUNK_BIAS_2 = 22
+CHUNK_MEAN = 23
+CHUNK_DEVIATIONS = 24
+CHUNK_NORMALISE = 25
 STEPS = TOKEN_TILES + CHUNK_NORMALISE
 
 
@@ -80,9 +78,9 @@ def tile_spatialmemorymodule_pb_kernel(
         packed = stack.enter_context(tc.tile_pool(name="packed", bufs=3))
         result = stack.enter_context(tc.tile_pool(name="result", bufs=3))
         psum_x = stack.enter_context(tc.psum_pool(name="psum_x", bufs=3))
-        psum_r = stack.enter_context(tc.psum_pool(name="psum_r", bufs=1))
+        psum_r = stack.enter_context(tc.psum_pool(name="psum_r", bufs=2))
         psum_h = stack.enter_context(tc.psum_pool(name="psum_h", bufs=2))
-        psum_t = stack.enter_context(tc.psum_pool(name="psum_t", bufs=2))
+        psum_z = stack.enter_context(tc.psum_pool(name="psum_z", bufs=1))
 
         z_sb = {}
 
@@ -100,25 +98,36 @@ def tile_spatialmemorymodule_pb_kernel(
         ident_f32 = const.tile([P, P], F32)
         make_identity(nc, ident_f32[:])
 
-        w1_words = const.tile([P, PASSES, PACK * HIDDEN], U8, align_bytes=64)
-        w1_planes = const.tile([P, PASSES, HIDDEN], U8, align_bytes=64)
+        w1_words_raw = const.tile([P, PASSES, PACK * HIDDEN], U8, align_bytes=64)
+        w1_planes_raw = const.tile([P, PASSES, HIDDEN], U8, align_bytes=64)
         w2_words = const.tile([P, 1, PACK * CODE], U8, align_bytes=64)
         w2_planes = const.tile([P, 1, CODE], U8, align_bytes=64)
-        nc.vector.memset(w1_planes[:].bitcast(I32), 0)
+        nc.vector.memset(w1_planes_raw[:].bitcast(I32), 0)
         nc.vector.memset(w2_planes[:].bitcast(I32), 0)
-        load_scale_rows(nc, w1_planes, Wq1_scales)
+        load_scale_rows(nc, w1_planes_raw, Wq1_scales)
         load_scale_rows(nc, w2_planes, Wq2_scales)
         nc.sync.dma_start(
-            out=w1_words[:].bitcast(I32), in_=Wq1_words.rearrange("g p n t -> p g (n t)").bitcast(I32)
+            out=w1_words_raw[:].bitcast(I32), in_=Wq1_words.rearrange("g p n t -> p g (n t)").bitcast(I32)
         )
         nc.sync.dma_start(
             out=w2_words[:].bitcast(I32), in_=Wq2_words.rearrange("g p n t -> p g (n t)").bitcast(I32)
         )
 
-        b1_rows = const.tile([P, HIDDEN], BF16)
-        nc.sync.dma_start(out=b1_rows[:], in_=bq1.partition_broadcast(P))
-        b1_by_t = const.tile([P, PACK, P], BF16)
-        nc.vector.tensor_copy(out=b1_by_t[:], in_=b1_rows[:].rearrange("q (p t) -> q t p", t=PACK))
+        w1_words = const.tile([P, PASSES, HIDDEN], I32, align_bytes=64)
+        w1_planes = const.tile([P, PASSES, HIDDEN], U8, align_bytes=64)
+        nc.vector.tensor_copy(
+            out=w1_words[:].rearrange("p g (t m) -> p g t m", t=PACK),
+            in_=w1_words_raw[:].bitcast(I32).rearrange("p g (m t) -> p g t m", t=PACK),
+        )
+        nc.vector.tensor_copy(
+            out=w1_planes[:].rearrange("p g (t m) -> p g m t", t=PACK),
+            in_=w1_planes_raw[:].rearrange("p g (m t) -> p g m t", t=PACK),
+        )
+
+        b1_loaded = const.tile([P, PACK], BF16)
+        nc.sync.dma_start(out=b1_loaded[:], in_=bq1.rearrange("(p t) -> p t", t=PACK))
+        b1_slots = const.tile([P, PACK], F32)
+        nc.vector.tensor_copy(out=b1_slots[:], in_=b1_loaded[:])
         b2_rows = const.tile([P, CODE], BF16)
         nc.sync.dma_start(out=b2_rows[:], in_=bq2.partition_broadcast(P))
 
@@ -128,8 +137,8 @@ def tile_spatialmemorymodule_pb_kernel(
         for c in range(1, Z_BUFFERS):
             load_chunk(c)
 
-        x_t, x_sumsq, x_inverse, inverse_rows, inverse_copy, xn, x_words, x_planes = {}, {}, {}, {}, {}, {}, {}, {}
-        h_sums, h_biased, h_t, h_grouped, h_words, h_planes = {}, {}, {}, {}, {}, {}
+        x_t, x_sumsq, x_inverse, inverse_rows, xn, x_words, x_planes = {}, {}, {}, {}, {}, {}, {}
+        h_sums, h_slots, h_grouped, h_words, h_planes = {}, {}, {}, {}, {}
         zq_sums, zq, minus_mean, dev_inverse = {}, {}, {}, {}
 
         def inverse_root(sums, floor):
@@ -161,7 +170,7 @@ def tile_spatialmemorymodule_pb_kernel(
             )
 
         def spread_inverse(c):
-            inverse_rows[c] = psum_r.tile([P, CHUNK], F32, name="inverse_rows", tag="shared")
+            inverse_rows[c] = psum_r.tile([P, CHUNK], F32, name="inverse_rows")
             for i in range(TILES):
                 nc.tensor.transpose(
                     inverse_rows[c][:, i * P : (i + 1) * P],
@@ -178,7 +187,7 @@ def tile_spatialmemorymodule_pb_kernel(
             nc.vector.tensor_tensor(
                 out=xn[c][:, g, first : first + count, :],
                 in0=z_sb[c][:, g, :, first : first + count].rearrange("p t x -> p x t"),
-                in1=inverse_copy[c][:, first : first + count].unsqueeze(2).to_broadcast([P, count, PACK]),
+                in1=inverse_rows[c][:, first : first + count].unsqueeze(2).to_broadcast([P, count, PACK]),
                 op=ALU.mult,
             )
 
@@ -192,44 +201,32 @@ def tile_spatialmemorymodule_pb_kernel(
                 in_=xn[c][:, g].rearrange("p x t -> p (x t)"),
             )
 
-        def product_1(k):
-            c, i = divmod(k, TILES)
-            h_sums[k] = psum_h.tile([P, HIDDEN], F32, name="h_sums")
+        def product_1(c, t):
+            h_sums[c, t] = psum_h.tile([P, CHUNK], F32, name="h_sums")
             for g in range(PASSES):
                 nc.tensor.matmul_mx(
-                    out=h_sums[k][:],
-                    lhsT=x_words[c][:, g, i * P : (i + 1) * P].bitcast(FP8X4),
-                    lhsT_scale=x_planes[c][:, g, i * P : (i + 1) * P],
-                    rhs=w1_words[:, g, :].bitcast(FP8X4),
-                    rhs_scale=w1_planes[:, g, :],
+                    out=h_sums[c, t][:],
+                    lhsT=w1_words[:, g, t * P : (t + 1) * P].bitcast(FP8X4),
+                    lhsT_scale=w1_planes[:, g, t * P : (t + 1) * P],
+                    rhs=x_words[c][:, g, :].bitcast(FP8X4),
+                    rhs_scale=x_planes[c][:, g, :],
                     start=(g == 0),
                     stop=(g == PASSES - 1),
                 )
 
-        def add_bias(k):
-            h_biased[k] = stage.tile([P, PACK, P], BF16, name="h_biased")
-            nc.vector.tensor_tensor(
-                out=h_biased[k][:],
-                in0=h_sums[k][:].rearrange("q (p t) -> q t p", t=PACK),
-                in1=b1_by_t[:],
-                op=ALU.add,
+        def relu_slot(c, t):
+            if t == 0:
+                h_slots[c] = stage.tile([P, PACK, CHUNK], BF16, name="h_slots")
+            nc.scalar.activation(
+                out=h_slots[c][:, t, :], in_=h_sums[c, t][:], func=ACT.Relu, bias=b1_slots[:, t : t + 1]
             )
 
-        def transpose_hidden(k):
-            pair, j = divmod(k, 2)
-            if j == 0:
-                h_t[pair] = psum_t.tile([P, 2, PACK, P], BF16, name="h_t")
-            for t in range(PACK):
-                nc.tensor.transpose(h_t[pair][:, j, t, :], h_biased[k][:, t, :], ident_bf[:])
-
-        def relu_pair(pair):
-            c, j = divmod(pair, TILES // 2)
-            if j == 0:
+        def group_hidden(c, i):
+            if i == 0:
                 h_grouped[c] = stage.tile([P, CHUNK, PACK], BF16, name="h_grouped", align_bytes=64)
-            nc.scalar.activation(
-                out=h_grouped[c][:, 2 * j * P : 2 * (j + 1) * P, :].rearrange("p (j n) t -> p j n t", j=2),
-                in_=h_t[pair][:].rearrange("p j t n -> p j n t"),
-                func=ACT.Relu,
+            nc.vector.tensor_copy(
+                out=h_grouped[c][:, i * P : (i + 1) * P, :],
+                in_=h_slots[c][:, :, i * P : (i + 1) * P].rearrange("p t n -> p n t"),
             )
 
         def quantise_h(c):
@@ -242,7 +239,7 @@ def tile_spatialmemorymodule_pb_kernel(
             )
 
         def product_2(c):
-            zq_sums[c] = psum_r.tile([P, TILES, CODE], F32, name="zq_sums", tag="shared")
+            zq_sums[c] = psum_z.tile([P, TILES, CODE], F32, name="zq_sums")
             for i in range(TILES):
                 nc.tensor.matmul_mx(
                     out=zq_sums[c][:, i, :],
@@ -303,9 +300,6 @@ def tile_spatialmemorymodule_pb_kernel(
             )
 
         for step in range(STEPS):
-            k = tile_due(step, TILE_BIAS)
-            if k is not None:
-                add_bias(k)
             c = chunk_due(step, CHUNK_BIAS_2)
             if c is not None:
                 add_bias_2(c)
@@ -313,15 +307,13 @@ def tile_spatialmemorymodule_pb_kernel(
             k = tile_due(step, 0)
             if k is not None:
                 transpose_tokens(k)
-            k = tile_due(step, TILE_TRANSPOSE_H)
-            if k is not None:
-                transpose_hidden(k)
             c = chunk_due(step, CHUNK_SPREAD)
             if c is not None:
                 spread_inverse(c)
-            k = tile_due(step, TILE_PRODUCT_1)
-            if k is not None:
-                product_1(k)
+            for t in range(PACK):
+                c = chunk_due(step, CHUNK_PRODUCT_1 + t)
+                if c is not None:
+                    product_1(c, t)
             c = chunk_due(step, CHUNK_PRODUCT_2)
             if c is not None:
                 product_2(c)
@@ -329,16 +321,13 @@ def tile_spatialmemorymodule_pb_kernel(
             k = tile_due(step, TILE_SQUARES)
             if k is not None:
                 sum_squares(k)
+            for t in range(PACK):
+                c = chunk_due(step, CHUNK_RELU + t)
+                if c is not None:
+                    relu_slot(c, t)
             c = chunk_due(step, CHUNK_INVERSE)
             if c is not None:
                 x_inverse[c] = inverse_root(x_sumsq[c][:], EPS * EPS)
-            c = chunk_due(step, CHUNK_COPY_INVERSE)
-            if c is not None:
-                inverse_copy[c] = stage.tile([P, CHUNK], F32, name="inverse_copy")
-                nc.scalar.copy(out=inverse_copy[c][:], in_=inverse_rows[c][:])
-            k = tile_due(step, TILE_RELU)
-            if k is not None and k % 2 == 1:
-                relu_pair(k // 2)
             c = chunk_due(step, CHUNK_MEAN)
             if c is not None:
                 mean(c)
@@ -352,6 +341,10 @@ def tile_spatialmemorymodule_pb_kernel(
                     scale_piece(c, piece)
                     if piece == 2 * PASSES - 1 and c + Z_BUFFERS < CHUNKS:
                         load_chunk(c + Z_BUFFERS)
+            for i in range(TILES):
+                c = chunk_due(step, CHUNK_GROUP_H + i)
+                if c is not None:
+                    group_hidden(c, i)
             for g in range(PASSES):
                 c = chunk_due(step, CHUNK_QUANTISE_X[g])
                 if c is not None:
@@ -364,7 +357,7 @@ def tile_spatialmemorymodule_pb_kernel(
             if c is not None:
                 normalise_and_store(c)
 
-        var_t = psum_r.tile([P, CHUNK], F32, tag="shared")
+        var_t = psum_z.tile([P, CHUNK], F32, name="zq_sums")
         nc.tensor.transpose(var_t[:, :P], dev_sumsq[:], ident_f32[:])
         var_rows = result.tile([P, P], F32)
         nc.vector.tensor_scalar_mul(out=var_rows[:], in0=var_t[:, :P], scalar1=1.0 / (CODE - 1))

@@ -139,7 +139,7 @@ def tile_spatialmemorymodule_pb_kernel(
 
         x_t, x_sumsq, x_inverse, inverse_rows, xn, x_words, x_planes = {}, {}, {}, {}, {}, {}, {}
         h_sums, h_slots, h_grouped, h_words, h_planes = {}, {}, {}, {}, {}
-        zq_sums, zq, minus_mean, dev_inverse = {}, {}, {}, {}
+        zq_sums, zq, zq_total, minus_mean, dev_inverse = {}, {}, {}, {}, {}
 
         def inverse_root(sums, floor):
             excess = small.tile([P, TILES], F32)
@@ -224,9 +224,13 @@ def tile_spatialmemorymodule_pb_kernel(
         def group_hidden(c, i):
             if i == 0:
                 h_grouped[c] = stage.tile([P, CHUNK, PACK], BF16, name="h_grouped", align_bytes=64)
-            nc.vector.tensor_copy(
+            nc.gpsimd.tensor_scalar(
                 out=h_grouped[c][:, i * P : (i + 1) * P, :],
-                in_=h_slots[c][:, :, i * P : (i + 1) * P].rearrange("p t n -> p n t"),
+                in0=h_slots[c][:, :, i * P : (i + 1) * P].rearrange("p t n -> p n t"),
+                scalar1=1.0,
+                scalar2=0.0,
+                op0=ALU.mult,
+                op1=ALU.add,
             )
 
         def quantise_h(c):
@@ -253,24 +257,21 @@ def tile_spatialmemorymodule_pb_kernel(
 
         def add_bias_2(c):
             zq[c] = result.tile([P, TILES, CODE], F32, name="zq")
-            nc.vector.tensor_tensor(
-                out=zq[c][:],
-                in0=zq_sums[c][:],
-                in1=b2_rows[:].unsqueeze(1).to_broadcast([P, TILES, CODE]),
-                op=ALU.add,
-            )
+            zq_total[c] = small.tile([P, TILES], F32, name="zq_total")
+            for i in range(TILES):
+                nc.vector.scalar_tensor_tensor(
+                    out=zq[c][:, i, :],
+                    in0=zq_sums[c][:, i, :],
+                    scalar=1.0,
+                    in1=b2_rows[:],
+                    op0=ALU.mult,
+                    op1=ALU.add,
+                    accum_out=zq_total[c][:, i : i + 1],
+                )
 
         def mean(c):
             minus_mean[c] = small.tile([P, TILES], F32, name="minus_mean")
-            for i in range(TILES):
-                shares = scrap.tile([P, CODE], F32)
-                nc.scalar.activation(
-                    out=shares[:],
-                    in_=zq[c][:, i, :],
-                    func=ACT.Identity,
-                    scale=-1.0 / CODE,
-                    accum_out=minus_mean[c][:, i : i + 1],
-                )
+            nc.vector.tensor_scalar_mul(out=minus_mean[c][:], in0=zq_total[c][:], scalar1=-1.0 / CODE)
 
         def sum_deviations(c):
             for i in range(TILES):
@@ -328,9 +329,6 @@ def tile_spatialmemorymodule_pb_kernel(
             c = chunk_due(step, CHUNK_INVERSE)
             if c is not None:
                 x_inverse[c] = inverse_root(x_sumsq[c][:], EPS * EPS)
-            c = chunk_due(step, CHUNK_MEAN)
-            if c is not None:
-                mean(c)
             c = chunk_due(step, CHUNK_DEVIATIONS)
             if c is not None:
                 sum_deviations(c)
@@ -341,10 +339,9 @@ def tile_spatialmemorymodule_pb_kernel(
                     scale_piece(c, piece)
                     if piece == 2 * PASSES - 1 and c + Z_BUFFERS < CHUNKS:
                         load_chunk(c + Z_BUFFERS)
-            for i in range(TILES):
-                c = chunk_due(step, CHUNK_GROUP_H + i)
-                if c is not None:
-                    group_hidden(c, i)
+            c = chunk_due(step, CHUNK_MEAN)
+            if c is not None:
+                mean(c)
             for g in range(PASSES):
                 c = chunk_due(step, CHUNK_QUANTISE_X[g])
                 if c is not None:
@@ -353,6 +350,10 @@ def tile_spatialmemorymodule_pb_kernel(
             if c is not None:
                 quantise_h(c)
 
+            for i in range(TILES):
+                c = chunk_due(step, CHUNK_GROUP_H + i)
+                if c is not None:
+                    group_hidden(c, i)
             c = chunk_due(step, CHUNK_NORMALISE)
             if c is not None:
                 normalise_and_store(c)

@@ -21,6 +21,7 @@ CHUNK = 512
 TILES = CHUNK // P
 CHUNKS = BATCH * PIXELS // CHUNK
 EPS = 1e-12
+RUN = 4
 
 FLOPS = 2 * BATCH * PIXELS * (CHANNELS * HIDDEN + HIDDEN * CODE)
 
@@ -185,9 +186,12 @@ def tile_spatialmemorymodule_pb_kernel(
             count = CHUNK // 2
             first = side * count
             nc.vector.tensor_tensor(
-                out=xn[c][:, g, first : first + count, :],
-                in0=z_sb[c][:, g, :, first : first + count].rearrange("p t x -> p x t"),
-                in1=inverse_rows[c][:, first : first + count].unsqueeze(2).to_broadcast([P, count, PACK]),
+                out=xn[c][:, g, first : first + count, :].rearrange("p (b i) t -> p b t i", i=RUN),
+                in0=z_sb[c][:, g, :, first : first + count].rearrange("p t (b i) -> p b t i", i=RUN),
+                in1=inverse_rows[c][:, first : first + count]
+                .rearrange("p (b i) -> p b i", i=RUN)
+                .unsqueeze(2)
+                .to_broadcast([P, count // RUN, PACK, RUN]),
                 op=ALU.mult,
             )
 

@@ -57,6 +57,10 @@ def chunk_due(step, lag):
     return k // TILES if k is not None and k % TILES == TILES - 1 else None
 
 
+def by_products(k):
+    return k % 2 == 0 and k % 16 != 14
+
+
 def load_scale_rows(nc, planes, scales):
     for quadrant in range(4):
         nc.sync.dma_start(
@@ -140,7 +144,7 @@ def tile_spatialmemorymodule_pb_kernel(
 
         x_t, x_sumsq, x_inverse, inverse_rows, xn, x_words, x_planes = {}, {}, {}, {}, {}, {}, {}
         h_sums, h_slots, h_grouped, h_words, h_planes = {}, {}, {}, {}, {}
-        zq_sums, zq, zq_total, minus_mean, dev_inverse = {}, {}, {}, {}, {}
+        zq_sums, zq, minus_mean, dev_inverse = {}, {}, {}, {}
 
         def inverse_root(sums, floor):
             excess = small.tile([P, TILES], F32)
@@ -158,10 +162,36 @@ def tile_spatialmemorymodule_pb_kernel(
                         x_t[k][:, g * PACK + t, :], z_sb[c][:, g, t, i * P : (i + 1) * P], ident_bf[:]
                     )
 
-        def sum_squares(k):
+        def multiply_tokens(k):
+            c, i = divmod(k, TILES)
+            x_t[k] = psum_x.tile([P, P], F32, name="x_t")
+            for s in range(PASSES * PACK):
+                g, t = divmod(s, PACK)
+                nc.tensor.matmul(
+                    out=x_t[k][:],
+                    lhsT=z_sb[c][:, g, t, i * P : (i + 1) * P],
+                    rhs=z_sb[c][:, g, t, i * P : (i + 1) * P],
+                    start=(s == 0),
+                    stop=(s == PASSES * PACK - 1),
+                )
+
+        def take_diagonal(k):
             c, i = divmod(k, TILES)
             if i == 0:
                 x_sumsq[c] = small.tile([P, TILES], F32, name="x_sumsq")
+            masked = scrap.tile([P, P], F32)
+            nc.vector.scalar_tensor_tensor(
+                out=masked[:],
+                in0=x_t[k][:],
+                scalar=1.0,
+                in1=ident_f32[:],
+                op0=ALU.mult,
+                op1=ALU.mult,
+                accum_out=x_sumsq[c][:, i : i + 1],
+            )
+
+        def sum_squares(k):
+            c, i = divmod(k, TILES)
             x_squares = scrap.tile([P, CHANNELS], BF16)
             nc.scalar.activation(
                 out=x_squares[:],
@@ -261,21 +291,24 @@ def tile_spatialmemorymodule_pb_kernel(
 
         def add_bias_2(c):
             zq[c] = result.tile([P, TILES, CODE], F32, name="zq")
-            zq_total[c] = small.tile([P, TILES], F32, name="zq_total")
-            for i in range(TILES):
-                nc.vector.scalar_tensor_tensor(
-                    out=zq[c][:, i, :],
-                    in0=zq_sums[c][:, i, :],
-                    scalar=1.0,
-                    in1=b2_rows[:],
-                    op0=ALU.mult,
-                    op1=ALU.add,
-                    accum_out=zq_total[c][:, i : i + 1],
-                )
+            nc.vector.tensor_tensor(
+                out=zq[c][:],
+                in0=zq_sums[c][:],
+                in1=b2_rows[:].unsqueeze(1).to_broadcast([P, TILES, CODE]),
+                op=ALU.add,
+            )
 
         def mean(c):
             minus_mean[c] = small.tile([P, TILES], F32, name="minus_mean")
-            nc.vector.tensor_scalar_mul(out=minus_mean[c][:], in0=zq_total[c][:], scalar1=-1.0 / CODE)
+            for i in range(TILES):
+                shares = scrap.tile([P, CODE], F32)
+                nc.scalar.activation(
+                    out=shares[:],
+                    in_=zq[c][:, i, :],
+                    func=ACT.Identity,
+                    scale=-1.0 / CODE,
+                    accum_out=minus_mean[c][:, i : i + 1],
+                )
 
         def sum_deviations(c):
             for i in range(TILES):
@@ -308,9 +341,14 @@ def tile_spatialmemorymodule_pb_kernel(
             c = chunk_due(step, CHUNK_BIAS_2)
             if c is not None:
                 add_bias_2(c)
+            k = tile_due(step, TILE_SQUARES)
+            if k is not None and by_products(k):
+                take_diagonal(k)
 
             k = tile_due(step, 0)
-            if k is not None:
+            if k is not None and by_products(k):
+                multiply_tokens(k)
+            if k is not None and not by_products(k):
                 transpose_tokens(k)
             c = chunk_due(step, CHUNK_SPREAD)
             if c is not None:
@@ -324,7 +362,7 @@ def tile_spatialmemorymodule_pb_kernel(
                 product_2(c)
 
             k = tile_due(step, TILE_SQUARES)
-            if k is not None:
+            if k is not None and not by_products(k):
                 sum_squares(k)
             for t in range(PACK):
                 c = chunk_due(step, CHUNK_RELU + t)
@@ -333,6 +371,9 @@ def tile_spatialmemorymodule_pb_kernel(
             c = chunk_due(step, CHUNK_INVERSE)
             if c is not None:
                 x_inverse[c] = inverse_root(x_sumsq[c][:], EPS * EPS)
+            c = chunk_due(step, CHUNK_MEAN)
+            if c is not None:
+                mean(c)
             c = chunk_due(step, CHUNK_DEVIATIONS)
             if c is not None:
                 sum_deviations(c)
@@ -343,9 +384,6 @@ def tile_spatialmemorymodule_pb_kernel(
                     scale_piece(c, piece)
                     if piece == 2 * PASSES - 1 and c + Z_BUFFERS < CHUNKS:
                         load_chunk(c + Z_BUFFERS)
-            c = chunk_due(step, CHUNK_MEAN)
-            if c is not None:
-                mean(c)
             for g in range(PASSES):
                 c = chunk_due(step, CHUNK_QUANTISE_X[g])
                 if c is not None:

@@ -17,48 +17,48 @@ PACK = 4
 BATCH, CHANNELS, PIXELS = 8, 1024, 1024
 HIDDEN, CODE = 512, 128
 PASSES = CHANNELS // (P * PACK)
-CHUNK = 512
-TILES = CHUNK // P
-CHUNKS = BATCH * PIXELS // CHUNK
+BLOCK = 512
+TILES = BLOCK // P
+BLOCKS = BATCH * PIXELS // BLOCK
+TOKEN_TILES = BATCH * PIXELS // P
+IMAGE_BLOCKS = PIXELS // BLOCK
+Z_BUFFERS = 6
 EPS = 1e-12
 RUN = 4
 
 FLOPS = 2 * BATCH * PIXELS * (CHANNELS * HIDDEN + HIDDEN * CODE)
 
-
-TOKEN_TILES = BATCH * PIXELS // P
-BATCH_CHUNKS = PIXELS // CHUNK
-Z_BUFFERS = 6
-
-TILE_SQUARES = 2
-CHUNK_INVERSE = 2
-CHUNK_SPREAD = 3
-CHUNK_SCALE = 5
-CHUNK_QUANTISE_X = (7, 9)
-CHUNK_PRODUCT_1 = 10
-CHUNK_RELU = 11
-CHUNK_GROUP_H = 15
-CHUNK_QUANTISE_H = 20
-CHUNK_PRODUCT_2 = 21
-CHUNK_BIAS_2 = 22
-CHUNK_MEAN = 23
-CHUNK_DEVIATIONS = 24
-CHUNK_NORMALISE = 25
-STEPS = TOKEN_TILES + CHUNK_NORMALISE
+V_FIRST = 0
+T_TOKENS = 1
+T_SPREAD = 2
+T_PRODUCT_1 = 3
+T_PRODUCT_2 = 4
+S_SQUARES = 5
+S_RELU = 6
+S_INVERSE = 7
+S_MEAN = 8
+S_DEVIATIONS = 9
+V_SCALE = 10
+V_GROUP = 11
+V_QUANTISE = 12
+G_GROUP = 13
+LAST = 14
 
 
-def tile_due(step, lag):
-    k = step - lag
-    return k if 0 <= k < TOKEN_TILES else None
-
-
-def chunk_due(step, lag):
-    k = tile_due(step, lag)
-    return k // TILES if k is not None and k % TILES == TILES - 1 else None
+def parts_of(c):
+    if c == 0:
+        return [(0, 1), (1, 1), (2, 2)]
+    if c == BLOCKS - 1:
+        return [(0, 2), (2, 1), (3, 1)]
+    return [(0, TILES)]
 
 
 def by_products(k):
     return k % 2 == 0 and k % 16 != 14
+
+
+def on_vector(c):
+    return c >= BLOCKS - 2
 
 
 def load_scale_rows(nc, planes, scales):
@@ -89,14 +89,19 @@ def tile_spatialmemorymodule_pb_kernel(
 
         z_sb = {}
 
-        def load_chunk(c):
-            b, half = divmod(c, BATCH_CHUNKS)
-            z_sb[c] = z_pool.tile([P, PASSES, PACK, CHUNK], BF16, name="z_sb")
-            for g in range(PASSES):
-                rows = z[b, g * P * PACK : (g + 1) * P * PACK].rearrange("(p t) h w -> p t (h w)", t=PACK)
-                nc.sync.dma_start(out=z_sb[c][:, g], in_=rows[:, :, half * CHUNK : (half + 1) * CHUNK])
+        def load_block(c):
+            b, place = divmod(c, IMAGE_BLOCKS)
+            z_sb[c] = z_pool.tile([P, PASSES, PACK, BLOCK], BF16, name="z_sb")
+            for i0, n in parts_of(c):
+                for g in range(PASSES):
+                    rows = z[b, g * P * PACK : (g + 1) * P * PACK].rearrange("(p t) h w -> p t (h w)", t=PACK)
+                    nc.sync.dma_start(
+                        out=z_sb[c][:, g, :, i0 * P : (i0 + n) * P],
+                        in_=rows[:, :, place * BLOCK + i0 * P : place * BLOCK + (i0 + n) * P],
+                    )
 
-        load_chunk(0)
+        load_block(0)
+        load_block(1)
 
         ident_bf = const.tile([P, P], BF16)
         make_identity(nc, ident_bf[:])
@@ -117,41 +122,46 @@ def tile_spatialmemorymodule_pb_kernel(
         nc.sync.dma_start(
             out=w2_words[:].bitcast(I32), in_=Wq2_words.rearrange("g p n t -> p g (n t)").bitcast(I32)
         )
-
-        w1_words = const.tile([P, PASSES, HIDDEN], I32, align_bytes=64)
-        w1_planes = const.tile([P, PASSES, HIDDEN], U8, align_bytes=64)
-        nc.vector.tensor_copy(
-            out=w1_words[:].rearrange("p g (t m) -> p g t m", t=PACK),
-            in_=w1_words_raw[:].bitcast(I32).rearrange("p g (m t) -> p g t m", t=PACK),
-        )
-        nc.vector.tensor_copy(
-            out=w1_planes[:].rearrange("p g (t m) -> p g m t", t=PACK),
-            in_=w1_planes_raw[:].rearrange("p g (m t) -> p g m t", t=PACK),
-        )
-
         b1_loaded = const.tile([P, PACK], BF16)
         nc.sync.dma_start(out=b1_loaded[:], in_=bq1.rearrange("(p t) -> p t", t=PACK))
-        b1_slots = const.tile([P, PACK], F32)
-        nc.vector.tensor_copy(out=b1_slots[:], in_=b1_loaded[:])
         b2_rows = const.tile([P, CODE], BF16)
         nc.sync.dma_start(out=b2_rows[:], in_=bq2.partition_broadcast(P))
+
+        for c in range(2, Z_BUFFERS):
+            load_block(c)
 
         dev_sumsq = const.tile([P, P], F32)
         nc.vector.memset(dev_sumsq[:], 0.0)
 
-        for c in range(1, Z_BUFFERS):
-            load_chunk(c)
+        w1_words = const.tile([P, PASSES, HIDDEN], I32, align_bytes=64)
+        w1_planes = const.tile([P, PASSES, HIDDEN], U8, align_bytes=64)
+        b1_slots = const.tile([P, PACK], F32)
 
-        x_t, x_sumsq, x_inverse, inverse_rows, xn, x_words, x_planes = {}, {}, {}, {}, {}, {}, {}
-        h_sums, h_slots, h_grouped, h_words, h_planes = {}, {}, {}, {}, {}
-        zq_sums, zq, minus_mean, dev_inverse = {}, {}, {}, {}
+        def reorder_weights():
+            nc.vector.tensor_copy(
+                out=w1_words[:].rearrange("p g (t m) -> p g t m", t=PACK),
+                in_=w1_words_raw[:].bitcast(I32).rearrange("p g (m t) -> p g t m", t=PACK),
+            )
+            nc.vector.tensor_copy(
+                out=w1_planes[:].rearrange("p g (t m) -> p g m t", t=PACK),
+                in_=w1_planes_raw[:].rearrange("p g (m t) -> p g m t", t=PACK),
+            )
+            nc.vector.tensor_copy(out=b1_slots[:], in_=b1_loaded[:])
 
-        def inverse_root(sums, floor):
+        x_t, inverse_rows, h_sums, zq_sums = {}, {}, {}, {}
+        x_sumsq, x_inverse, xn, x_words, x_planes = {}, {}, {}, {}, {}
+        h_slots, h_grouped, h_words, h_planes = {}, {}, {}, {}
+        zq, zc, minus_mean, dev_inverse = {}, {}, {}, {}
+
+        def of_block(kept, c, pool, shape, dtype, name):
+            if c not in kept:
+                kept[c] = pool.tile(shape, dtype, name=name, align_bytes=64)
+            return kept[c]
+
+        def inverse_root(out, sums, floor, n):
             excess = small.tile([P, TILES], F32)
-            nc.scalar.activation(out=excess[:], in_=sums, func=ACT.Relu, bias=-floor)
-            inverse = small.tile([P, TILES], F32)
-            nc.scalar.activation(out=inverse[:], in_=excess[:], func=ACT.Abs_reciprocal_sqrt, bias=floor)
-            return inverse
+            nc.scalar.activation(out=excess[:, :n], in_=sums, func=ACT.Relu, bias=-floor)
+            nc.scalar.activation(out=out, in_=excess[:, :n], func=ACT.Abs_reciprocal_sqrt, bias=floor)
 
         def transpose_tokens(k):
             c, i = divmod(k, TILES)
@@ -161,6 +171,17 @@ def tile_spatialmemorymodule_pb_kernel(
                     nc.tensor.transpose(
                         x_t[k][:, g * PACK + t, :], z_sb[c][:, g, t, i * P : (i + 1) * P], ident_bf[:]
                     )
+
+        def sum_squares(k):
+            c, i = divmod(k, TILES)
+            sums = of_block(x_sumsq, c, small, [P, TILES], F32, "x_sumsq")
+            x_squares = scrap.tile([P, CHANNELS], BF16)
+            nc.scalar.activation(
+                out=x_squares[:],
+                in_=x_t[k][:].rearrange("q a c -> q (a c)"),
+                func=ACT.Square,
+                accum_out=sums[:, i : i + 1],
+            )
 
         def multiply_tokens(k):
             c, i = divmod(k, TILES)
@@ -177,8 +198,7 @@ def tile_spatialmemorymodule_pb_kernel(
 
         def take_diagonal(k):
             c, i = divmod(k, TILES)
-            if i == 0:
-                x_sumsq[c] = small.tile([P, TILES], F32, name="x_sumsq")
+            sums = of_block(x_sumsq, c, small, [P, TILES], F32, "x_sumsq")
             masked = scrap.tile([P, P], F32)
             nc.vector.scalar_tensor_tensor(
                 out=masked[:],
@@ -187,131 +207,135 @@ def tile_spatialmemorymodule_pb_kernel(
                 in1=ident_f32[:],
                 op0=ALU.mult,
                 op1=ALU.mult,
-                accum_out=x_sumsq[c][:, i : i + 1],
+                accum_out=sums[:, i : i + 1],
             )
 
-        def sum_squares(k):
-            c, i = divmod(k, TILES)
-            x_squares = scrap.tile([P, CHANNELS], BF16)
-            nc.scalar.activation(
-                out=x_squares[:],
-                in_=x_t[k][:].rearrange("q a c -> q (a c)"),
-                func=ACT.Square,
-                accum_out=x_sumsq[c][:, i : i + 1],
-            )
+        def invert_norms(c, i0, n):
+            inverse = of_block(x_inverse, c, small, [P, TILES], F32, "x_inverse")
+            inverse_root(inverse[:, i0 : i0 + n], x_sumsq[c][:, i0 : i0 + n], EPS * EPS, n)
 
-        def spread_inverse(c):
-            inverse_rows[c] = psum_r.tile([P, CHUNK], F32, name="inverse_rows")
-            for i in range(TILES):
+        def spread_inverse(c, i0, n):
+            inverse_rows[c, i0] = psum_r.tile([P, n * P], F32, name="inverse_rows")
+            for i in range(n):
                 nc.tensor.transpose(
-                    inverse_rows[c][:, i * P : (i + 1) * P],
-                    x_inverse[c][:, i : i + 1].to_broadcast([P, P]),
+                    inverse_rows[c, i0][:, i * P : (i + 1) * P],
+                    x_inverse[c][:, i0 + i : i0 + i + 1].to_broadcast([P, P]),
                     ident_f32[:],
                 )
 
-        def scale_piece(c, piece):
-            g, side = divmod(piece, 2)
-            if piece == 0:
-                xn[c] = stage.tile([P, PASSES, CHUNK, PACK], BF16, name="xn", align_bytes=64)
-            count = CHUNK // 2
-            first = side * count
+        def scale_piece(c, i0, g, first, count):
+            scaled = of_block(xn, c, stage, [P, PASSES, BLOCK, PACK], BF16, "xn")
+            at = i0 * P + first
             nc.vector.tensor_tensor(
-                out=xn[c][:, g, first : first + count, :].rearrange("p (b i) t -> p b t i", i=RUN),
-                in0=z_sb[c][:, g, :, first : first + count].rearrange("p t (b i) -> p b t i", i=RUN),
-                in1=inverse_rows[c][:, first : first + count]
+                out=scaled[:, g, at : at + count, :].rearrange("p (b i) t -> p b t i", i=RUN),
+                in0=z_sb[c][:, g, :, at : at + count].rearrange("p t (b i) -> p b t i", i=RUN),
+                in1=inverse_rows[c, i0][:, first : first + count]
                 .rearrange("p (b i) -> p b i", i=RUN)
                 .unsqueeze(2)
                 .to_broadcast([P, count // RUN, PACK, RUN]),
                 op=ALU.mult,
             )
 
-        def quantise_x(c, g):
-            if g == 0:
-                x_words[c] = packed.tile([P, PASSES, CHUNK], U32, name="x_words", align_bytes=64)
-                x_planes[c] = packed.tile([P, PASSES, CHUNK], U8, name="x_planes", align_bytes=64)
+        def quantise_x(c, i0, n, g):
+            words = of_block(x_words, c, packed, [P, PASSES, BLOCK], U32, "x_words")
+            planes = of_block(x_planes, c, packed, [P, PASSES, BLOCK], U8, "x_planes")
             nc.vector.quantize_mx(
-                out=x_words[c][:, g, :].bitcast(FP8X4),
-                scales=x_planes[c][:, g, :],
-                in_=xn[c][:, g].rearrange("p x t -> p (x t)"),
+                out=words[:, g, i0 * P : (i0 + n) * P].bitcast(FP8X4),
+                scales=planes[:, g, i0 * P : (i0 + n) * P],
+                in_=xn[c][:, g, i0 * P : (i0 + n) * P, :].rearrange("p x t -> p (x t)"),
             )
 
-        def product_1(c, t):
-            h_sums[c, t] = psum_h.tile([P, CHUNK], F32, name="h_sums")
-            for g in range(PASSES):
-                nc.tensor.matmul_mx(
-                    out=h_sums[c, t][:],
-                    lhsT=w1_words[:, g, t * P : (t + 1) * P].bitcast(FP8X4),
-                    lhsT_scale=w1_planes[:, g, t * P : (t + 1) * P],
-                    rhs=x_words[c][:, g, :].bitcast(FP8X4),
-                    rhs_scale=x_planes[c][:, g, :],
-                    start=(g == 0),
-                    stop=(g == PASSES - 1),
+        def product_1(c, i0, n, u):
+            slots = TILES // n
+            h_sums[c, i0, u] = psum_h.tile([P, slots, n * P], F32, name="h_sums")
+            for s in range(slots):
+                t = u * slots + s
+                for g in range(PASSES):
+                    nc.tensor.matmul_mx(
+                        out=h_sums[c, i0, u][:, s, :],
+                        lhsT=w1_words[:, g, t * P : (t + 1) * P].bitcast(FP8X4),
+                        lhsT_scale=w1_planes[:, g, t * P : (t + 1) * P],
+                        rhs=x_words[c][:, g, i0 * P : (i0 + n) * P].bitcast(FP8X4),
+                        rhs_scale=x_planes[c][:, g, i0 * P : (i0 + n) * P],
+                        start=(g == 0),
+                        stop=(g == PASSES - 1),
+                    )
+
+        def relu_bank(c, i0, n, u):
+            slots = TILES // n
+            kept = of_block(h_slots, c, stage, [P, PACK, BLOCK], BF16, "h_slots")
+            for s in range(slots):
+                t = u * slots + s
+                nc.scalar.activation(
+                    out=kept[:, t, i0 * P : (i0 + n) * P],
+                    in_=h_sums[c, i0, u][:, s, :],
+                    func=ACT.Relu,
+                    bias=b1_slots[:, t : t + 1],
                 )
 
-        def relu_slot(c, t):
-            if t == 0:
-                h_slots[c] = stage.tile([P, PACK, CHUNK], BF16, name="h_slots")
-            nc.scalar.activation(
-                out=h_slots[c][:, t, :], in_=h_sums[c, t][:], func=ACT.Relu, bias=b1_slots[:, t : t + 1]
-            )
-
         def group_hidden(c, i):
-            if i == 0:
-                h_grouped[c] = stage.tile([P, CHUNK, PACK], BF16, name="h_grouped", align_bytes=64)
-            nc.gpsimd.tensor_scalar(
-                out=h_grouped[c][:, i * P : (i + 1) * P, :],
-                in0=h_slots[c][:, :, i * P : (i + 1) * P].rearrange("p t n -> p n t"),
-                scalar1=1.0,
-                scalar2=0.0,
-                op0=ALU.mult,
-                op1=ALU.add,
-            )
+            grouped = of_block(h_grouped, c, stage, [P, BLOCK, PACK], BF16, "h_grouped")
+            if on_vector(c):
+                nc.vector.tensor_copy(
+                    out=grouped[:, i * P : (i + 1) * P, :],
+                    in_=h_slots[c][:, :, i * P : (i + 1) * P].rearrange("p t n -> p n t"),
+                )
+            else:
+                nc.gpsimd.tensor_scalar(
+                    out=grouped[:, i * P : (i + 1) * P, :],
+                    in0=h_slots[c][:, :, i * P : (i + 1) * P].rearrange("p t n -> p n t"),
+                    scalar1=1.0,
+                    scalar2=0.0,
+                    op0=ALU.mult,
+                    op1=ALU.add,
+                )
 
-        def quantise_h(c):
-            h_words[c] = packed.tile([P, CHUNK], U32, name="h_words", align_bytes=64)
-            h_planes[c] = packed.tile([P, CHUNK], U8, name="h_planes", align_bytes=64)
+        def quantise_h(c, i0, n):
+            words = of_block(h_words, c, packed, [P, BLOCK], U32, "h_words")
+            planes = of_block(h_planes, c, packed, [P, BLOCK], U8, "h_planes")
             nc.vector.quantize_mx(
-                out=h_words[c][:].bitcast(FP8X4),
-                scales=h_planes[c][:],
-                in_=h_grouped[c][:].rearrange("p n t -> p (n t)"),
+                out=words[:, i0 * P : (i0 + n) * P].bitcast(FP8X4),
+                scales=planes[:, i0 * P : (i0 + n) * P],
+                in_=h_grouped[c][:, i0 * P : (i0 + n) * P, :].rearrange("p n t -> p (n t)"),
             )
 
-        def product_2(c):
-            zq_sums[c] = psum_z.tile([P, TILES, CODE], F32, name="zq_sums")
-            for i in range(TILES):
+        def product_2(c, i0, n):
+            zq_sums[c, i0] = psum_z.tile([P, n, CODE], F32, name="zq_sums")
+            for i in range(n):
                 nc.tensor.matmul_mx(
-                    out=zq_sums[c][:, i, :],
-                    lhsT=h_words[c][:, i * P : (i + 1) * P].bitcast(FP8X4),
-                    lhsT_scale=h_planes[c][:, i * P : (i + 1) * P],
+                    out=zq_sums[c, i0][:, i, :],
+                    lhsT=h_words[c][:, (i0 + i) * P : (i0 + i + 1) * P].bitcast(FP8X4),
+                    lhsT_scale=h_planes[c][:, (i0 + i) * P : (i0 + i + 1) * P],
                     rhs=w2_words[:, 0, :].bitcast(FP8X4),
                     rhs_scale=w2_planes[:, 0, :],
                     start=True,
                     stop=True,
                 )
 
-        def add_bias_2(c):
-            zq[c] = result.tile([P, TILES, CODE], F32, name="zq")
+        def add_bias_2(c, i0, n):
+            kept = of_block(zq, c, result, [P, TILES, CODE], F32, "zq")
             nc.vector.tensor_tensor(
-                out=zq[c][:],
-                in0=zq_sums[c][:],
-                in1=b2_rows[:].unsqueeze(1).to_broadcast([P, TILES, CODE]),
+                out=kept[:, i0 : i0 + n, :],
+                in0=zq_sums[c, i0][:],
+                in1=b2_rows[:].unsqueeze(1).to_broadcast([P, n, CODE]),
                 op=ALU.add,
             )
 
-        def mean(c):
-            minus_mean[c] = small.tile([P, TILES], F32, name="minus_mean")
-            for i in range(TILES):
+        def mean(c, i0, n):
+            kept = of_block(minus_mean, c, small, [P, TILES], F32, "minus_mean")
+            for i in range(i0, i0 + n):
                 shares = scrap.tile([P, CODE], F32)
                 nc.scalar.activation(
                     out=shares[:],
                     in_=zq[c][:, i, :],
                     func=ACT.Identity,
                     scale=-1.0 / CODE,
-                    accum_out=minus_mean[c][:, i : i + 1],
+                    accum_out=kept[:, i : i + 1],
                 )
 
-        def sum_deviations(c):
-            for i in range(TILES):
+        def sum_deviations(c, i0, n):
+            first = c * TILES + i0
+            for i in range(i0, i0 + n):
                 dev_squares = scrap.tile([P, CODE], F32)
                 nc.scalar.activation(
                     out=dev_squares[:],
@@ -320,88 +344,83 @@ def tile_spatialmemorymodule_pb_kernel(
                     bias=minus_mean[c][:, i : i + 1],
                     accum_out=dev_sumsq[:, c * TILES + i : c * TILES + i + 1],
                 )
-            dev_inverse[c] = inverse_root(dev_sumsq[:, c * TILES : (c + 1) * TILES], EPS * EPS)
+            inverse = of_block(dev_inverse, c, small, [P, TILES], F32, "dev_inverse")
+            inverse_root(inverse[:, i0 : i0 + n], dev_sumsq[:, first : first + n], EPS * EPS, n)
 
-        def normalise_and_store(c):
-            zc = result.tile([P, TILES, CODE], F32)
-            for i in range(TILES):
-                nc.gpsimd.tensor_scalar(
-                    out=zc[:, i, :],
+        def normalise_and_store(c, i0, n):
+            kept = of_block(zc, c, result, [P, TILES, CODE], F32, "zc")
+            engine = nc.vector if on_vector(c) else nc.gpsimd
+            for i in range(i0, i0 + n):
+                engine.tensor_scalar(
+                    out=kept[:, i, :],
                     in0=zq[c][:, i, :],
                     scalar1=minus_mean[c][:, i : i + 1],
                     scalar2=dev_inverse[c][:, i : i + 1],
                     op0=ALU.add,
                     op1=ALU.mult,
                 )
+            first = c * BLOCK + i0 * P
             nc.sync.dma_start(
-                out=out_0[c * CHUNK : (c + 1) * CHUNK, :].rearrange("(i q) d -> q i d", q=P), in_=zc[:]
+                out=out_0[first : first + n * P, :].rearrange("(i q) d -> q i d", q=P),
+                in_=kept[:, i0 : i0 + n, :],
             )
 
-        for step in range(STEPS):
-            c = chunk_due(step, CHUNK_BIAS_2)
-            if c is not None:
-                add_bias_2(c)
-            k = tile_due(step, TILE_SQUARES)
-            if k is not None and by_products(k):
-                take_diagonal(k)
+        booked = []
 
-            k = tile_due(step, 0)
-            if k is not None and by_products(k):
-                multiply_tokens(k)
-            if k is not None and not by_products(k):
-                transpose_tokens(k)
-            c = chunk_due(step, CHUNK_SPREAD)
-            if c is not None:
-                spread_inverse(c)
-            for t in range(PACK):
-                c = chunk_due(step, CHUNK_PRODUCT_1 + t)
-                if c is not None:
-                    product_1(c, t)
-            c = chunk_due(step, CHUNK_PRODUCT_2)
-            if c is not None:
-                product_2(c)
+        def book(step, rank, stage_function, *arguments):
+            booked.append((step, rank, len(booked), stage_function, arguments))
 
-            k = tile_due(step, TILE_SQUARES)
-            if k is not None and not by_products(k):
-                sum_squares(k)
-            for t in range(PACK):
-                c = chunk_due(step, CHUNK_RELU + t)
-                if c is not None:
-                    relu_slot(c, t)
-            c = chunk_due(step, CHUNK_INVERSE)
-            if c is not None:
-                x_inverse[c] = inverse_root(x_sumsq[c][:], EPS * EPS)
-            c = chunk_due(step, CHUNK_MEAN)
-            if c is not None:
-                mean(c)
-            c = chunk_due(step, CHUNK_DEVIATIONS)
-            if c is not None:
-                sum_deviations(c)
+        book(6, V_GROUP, reorder_weights)
+        for k in range(TOKEN_TILES):
+            if by_products(k):
+                book(k, T_TOKENS, multiply_tokens, k)
+                book(k + 2, V_FIRST, take_diagonal, k)
+            else:
+                book(k, T_TOKENS, transpose_tokens, k)
+                book(k + 2, S_SQUARES, sum_squares, k)
 
-            for piece in range(2 * PASSES):
-                c = chunk_due(step, CHUNK_SCALE + piece)
-                if c is not None:
-                    scale_piece(c, piece)
-                    if piece == 2 * PASSES - 1 and c + Z_BUFFERS < CHUNKS:
-                        load_chunk(c + Z_BUFFERS)
-            for g in range(PASSES):
-                c = chunk_due(step, CHUNK_QUANTISE_X[g])
-                if c is not None:
-                    quantise_x(c, g)
-            c = chunk_due(step, CHUNK_QUANTISE_H)
-            if c is not None:
-                quantise_h(c)
+        scaled_at = [0, 0]
+        bank_free = group_free = bias_2_at = 0
+        for c in range(BLOCKS):
+            for i0, n in parts_of(c):
+                step = c * TILES + i0 + n - 1
+                book(step + 2, S_INVERSE, invert_norms, c, i0, n)
+                step = max(step + 3, scaled_at[-2] + 1)
+                book(step, T_SPREAD, spread_inverse, c, i0, n)
+                step = max(step + 2, scaled_at[-1] + 1)
+                count = min(n * P, 2 * P)
+                pieces = [(g, first) for g in range(PASSES) for first in range(0, n * P, count)]
+                for u, (g, first) in enumerate(pieces):
+                    book(step + u * n // len(pieces), V_SCALE, scale_piece, c, i0, g, first, count)
+                scaled_at.append(step + n - 1)
+                if i0 + n == TILES and c + Z_BUFFERS < BLOCKS:
+                    book(step + n - 1, V_GROUP, load_block, c + Z_BUFFERS)
+                for g in range(PASSES):
+                    book(step + max(1, (g + 1) * n // PASSES), V_QUANTISE, quantise_x, c, i0, n, g)
+                step = max(step + n + 1, bank_free)
+                for u in range(n):
+                    book(step + u, T_PRODUCT_1, product_1, c, i0, n, u)
+                    book(step + u + 1, S_RELU, relu_bank, c, i0, n, u)
+                bank_free = step + n
+                step = max(step + n + 1, group_free)
+                for i in range(n):
+                    book(step + i, V_GROUP if on_vector(c) else G_GROUP, group_hidden, c, i0 + i)
+                group_free = step + n
+                step = step + n if on_vector(c) else step + n + 1
+                book(step, V_QUANTISE, quantise_h, c, i0, n)
+                step = max(step + 1, bias_2_at)
+                book(step, T_PRODUCT_2, product_2, c, i0, n)
+                bias_2_at = step + 1
+                book(step + 1, V_FIRST, add_bias_2, c, i0, n)
+                book(step + 2, S_MEAN, mean, c, i0, n)
+                book(step + 3, S_DEVIATIONS, sum_deviations, c, i0, n)
+                book(step + 4, LAST, normalise_and_store, c, i0, n)
 
-            for i in range(TILES):
-                c = chunk_due(step, CHUNK_GROUP_H + i)
-                if c is not None:
-                    group_hidden(c, i)
-            c = chunk_due(step, CHUNK_NORMALISE)
-            if c is not None:
-                normalise_and_store(c)
+        for step, rank, serial, stage_function, arguments in sorted(booked):
+            stage_function(*arguments)
 
-        var_t = psum_z.tile([P, CHUNK], F32, name="zq_sums")
-        nc.tensor.transpose(var_t[:, :P], dev_sumsq[:], ident_f32[:])
+        var_t = psum_z.tile([P, P], F32, name="zq_sums")
+        nc.tensor.transpose(var_t[:], dev_sumsq[:], ident_f32[:])
         var_rows = result.tile([P, P], F32)
-        nc.vector.tensor_scalar_mul(out=var_rows[:], in0=var_t[:, :P], scalar1=1.0 / (CODE - 1))
+        nc.vector.tensor_scalar_mul(out=var_rows[:], in0=var_t[:], scalar1=1.0 / (CODE - 1))
         nc.sync.dma_start(out=out_1.rearrange("(i q) o -> i (q o)", q=P), in_=var_rows[:TOKEN_TILES, :])

from contextlib import ExitStack

import concourse.mybir as mybir
from concourse.masks import make_identity

BF16 = mybir.dt.bfloat16
F32 = mybir.dt.float32
I32 = mybir.dt.int32
U8 = mybir.dt.uint8
U32 = mybir.dt.uint32
FP8X4 = mybir.dt.float8_e4m3fn_x4
ACT = mybir.ActivationFunctionType
ALU = mybir.AluOpType

P = 128
PACK = 4
BATCH, CHANNELS, PIXELS = 8, 1024, 1024
HIDDEN, CODE = 512, 128
PASSES = CHANNELS // (P * PACK)
BLOCK = 512
TILES = BLOCK // P
BLOCKS = BATCH * PIXELS // BLOCK
TOKEN_TILES = BATCH * PIXELS // P
IMAGE_BLOCKS = PIXELS // BLOCK
Z_BUFFERS = 6
EPS = 1e-12
RUN = 4

FLOPS = 2 * BATCH * PIXELS * (CHANNELS * HIDDEN + HIDDEN * CODE)

V_FIRST = 0
T_TOKENS = 1
T_SPREAD = 2
T_PRODUCT_1 = 3
T_PRODUCT_2 = 4
S_SQUARES = 5
S_RELU = 6
S_INVERSE = 7
S_MEAN = 8
S_DEVIATIONS = 9
V_SCALE = 10
V_GROUP = 11
V_QUANTISE = 12
G_GROUP = 13
LAST = 14


def parts_of(c):
    if c == 0:
        return [(0, 1), (1, 1), (2, 2)]
    if c == BLOCKS - 1:
        return [(0, 2), (2, 1), (3, 1)]
    return [(0, TILES)]


def by_products(k):
    return k % 2 == 0 and k % 16 != 14


def on_vector(c):
    return c >= BLOCKS - 2


def load_scale_rows(nc, planes, scales):
    for quadrant in range(4):
        nc.sync.dma_start(
            out=planes[32 * quadrant : 32 * quadrant + 4].bitcast(I32),
            in_=scales[:, 4 * quadrant : 4 * quadrant + 4, :].rearrange("g r n -> r g n").bitcast(I32),
        )


def tile_spatialmemorymodule_pb_kernel(
    tc, z, Wq1_words, Wq1_scales, bq1, Wq2_words, Wq2_scales, bq2, out_0, out_1
):
    nc = tc.nc
    with ExitStack() as stack:
        stack.enter_context(tc.manual_schedule())
        const = stack.enter_context(tc.tile_pool(name="const", bufs=1))
        z_pool = stack.enter_context(tc.tile_pool(name="z", bufs=Z_BUFFERS))
        scrap = stack.enter_context(tc.tile_pool(name="scrap", bufs=4))
        small = stack.enter_context(tc.tile_pool(name="small", bufs=4))
        stage = stack.enter_context(tc.tile_pool(name="stage", bufs=4))
        packed = stack.enter_context(tc.tile_pool(name="packed", bufs=3))
        result = stack.enter_context(tc.tile_pool(name="result", bufs=3))
        psum_x = stack.enter_context(tc.psum_pool(name="psum_x", bufs=3))
        psum_r = stack.enter_context(tc.psum_pool(name="psum_r", bufs=2))
        psum_h = stack.enter_context(tc.psum_pool(name="psum_h", bufs=2))
        psum_z = stack.enter_context(tc.psum_pool(name="psum_z", bufs=1))

        z_sb = {}

        def load_block(c):
            b, place = divmod(c, IMAGE_BLOCKS)
            z_sb[c] = z_pool.tile([P, PASSES, PACK, BLOCK], BF16, name="z_sb")
            for i0, n in parts_of(c):
                for g in range(PASSES):
                    rows = z[b, g * P * PACK : (g + 1) * P * PACK].rearrange("(p t) h w -> p t (h w)", t=PACK)
                    nc.sync.dma_start(
                        out=z_sb[c][:, g, :, i0 * P : (i0 + n) * P],
                        in_=rows[:, :, place * BLOCK + i0 * P : place * BLOCK + (i0 + n) * P],
                    )

        load_block(0)
        load_block(1)

        ident_bf = const.tile([P, P], BF16)
        make_identity(nc, ident_bf[:])
        ident_f32 = const.tile([P, P], F32)
        make_identity(nc, ident_f32[:])

        w1_words_raw = const.tile([P, PASSES, PACK * HIDDEN], U8, align_bytes=64)
        w1_planes_raw = const.tile([P, PASSES, HIDDEN], U8, align_bytes=64)
        w2_words = const.tile([P, 1, PACK * CODE], U8, align_bytes=64)
        w2_planes = const.tile([P, 1, CODE], U8, align_bytes=64)
        nc.vector.memset(w1_planes_raw[:].bitcast(I32), 0)
        nc.vector.memset(w2_planes[:].bitcast(I32), 0)
        load_scale_rows(nc, w1_planes_raw, Wq1_scales)
        load_scale_rows(nc, w2_planes, Wq2_scales)
        nc.sync.dma_start(
            out=w1_words_raw[:].bitcast(I32), in_=Wq1_words.rearrange("g p n t -> p g (n t)").bitcast(I32)
        )
        nc.sync.dma_start(
            out=w2_words[:].bitcast(I32), in_=Wq2_words.rearrange("g p n t -> p g (n t)").bitcast(I32)
        )
        b1_loaded = const.tile([P, PACK], BF16)
        nc.sync.dma_start(out=b1_loaded[:], in_=bq1.rearrange("(p t) -> p t", t=PACK))
        b2_rows = const.tile([P, CODE], BF16)
        nc.sync.dma_start(out=b2_rows[:], in_=bq2.partition_broadcast(P))

        for c in range(2, Z_BUFFERS):
            load_block(c)

        dev_sumsq = const.tile([P, P], F32)
        nc.vector.memset(dev_sumsq[:], 0.0)

        w1_words = const.tile([P, PASSES, HIDDEN], I32, align_bytes=64)
        w1_planes = const.tile([P, PASSES, HIDDEN], U8, align_bytes=64)
        b1_slots = const.tile([P, PACK], F32)

        def reorder_weights():
            nc.vector.tensor_copy(
                out=w1_words[:].rearrange("p g (t m) -> p g t m", t=PACK),
                in_=w1_words_raw[:].bitcast(I32).rearrange("p g (m t) -> p g t m", t=PACK),
            )
            nc.vector.tensor_copy(
                out=w1_planes[:].rearrange("p g (t m) -> p g m t", t=PACK),
                in_=w1_planes_raw[:].rearrange("p g (m t) -> p g m t", t=PACK),
            )
            nc.vector.tensor_copy(out=b1_slots[:], in_=b1_loaded[:])

        x_t, inverse_rows, h_sums, zq_sums = {}, {}, {}, {}
        x_sumsq, x_inverse, xn, x_words, x_planes = {}, {}, {}, {}, {}
        h_slots, h_grouped, h_words, h_planes = {}, {}, {}, {}
        zq, zc, minus_mean, dev_inverse = {}, {}, {}, {}

        def of_block(kept, c, pool, shape, dtype, name):
            if c not in kept:
                kept[c] = pool.tile(shape, dtype, name=name, align_bytes=64)
            return kept[c]

        def inverse_root(out, sums, floor, n):
            excess = small.tile([P, TILES], F32)
            nc.scalar.activation(out=excess[:, :n], in_=sums, func=ACT.Relu, bias=-floor)
            nc.scalar.activation(out=out, in_=excess[:, :n], func=ACT.Abs_reciprocal_sqrt, bias=floor)

        def transpose_tokens(k):
            c, i = divmod(k, TILES)
            x_t[k] = psum_x.tile([P, PASSES * PACK, P], BF16, name="x_t")
            for g in range(PASSES):
                for t in range(PACK):
                    nc.tensor.transpose(
                        x_t[k][:, g * PACK + t, :], z_sb[c][:, g, t, i * P : (i + 1) * P], ident_bf[:]
                    )

        def sum_squares(k):
            c, i = divmod(k, TILES)
            sums = of_block(x_sumsq, c, small, [P, TILES], F32, "x_sumsq")
            x_squares = scrap.tile([P, CHANNELS], BF16)
            nc.scalar.activation(
                out=x_squares[:],
                in_=x_t[k][:].rearrange("q a c -> q (a c)"),
                func=ACT.Square,
                accum_out=sums[:, i : i + 1],
            )

        def multiply_tokens(k):
            c, i = divmod(k, TILES)
            x_t[k] = psum_x.tile([P, P], F32, name="x_t")
            for s in range(PASSES * PACK):
                g, t = divmod(s, PACK)
                nc.tensor.matmul(
                    out=x_t[k][:],
                    lhsT=z_sb[c][:, g, t, i * P : (i + 1) * P],
                    rhs=z_sb[c][:, g, t, i * P : (i + 1) * P],
                    start=(s == 0),
                    stop=(s == PASSES * PACK - 1),
                )

        def take_diagonal(k):
            c, i = divmod(k, TILES)
            sums = of_block(x_sumsq, c, small, [P, TILES], F32, "x_sumsq")
            masked = scrap.tile([P, P], F32)
            nc.vector.scalar_tensor_tensor(
                out=masked[:],
                in0=x_t[k][:],
                scalar=1.0,
                in1=ident_f32[:],
                op0=ALU.mult,
                op1=ALU.mult,
                accum_out=sums[:, i : i + 1],
            )

        def invert_norms(c, i0, n):
            inverse = of_block(x_inverse, c, small, [P, TILES], F32, "x_inverse")
            inverse_root(inverse[:, i0 : i0 + n], x_sumsq[c][:, i0 : i0 + n], EPS * EPS, n)

        def spread_inverse(c, i0, n):
            inverse_rows[c, i0] = psum_r.tile([P, n * P], F32, name="inverse_rows")
            for i in range(n):
                nc.tensor.transpose(
                    inverse_rows[c, i0][:, i * P : (i + 1) * P],
                    x_inverse[c][:, i0 + i : i0 + i + 1].to_broadcast([P, P]),
                    ident_f32[:],
                )

        def scale_piece(c, i0, g, first, count):
            scaled = of_block(xn, c, stage, [P, PASSES, BLOCK, PACK], BF16, "xn")
            at = i0 * P + first
            nc.vector.tensor_tensor(
                out=scaled[:, g, at : at + count, :].rearrange("p (b i) t -> p b t i", i=RUN),
                in0=z_sb[c][:, g, :, at : at + count].rearrange("p t (b i) -> p b t i", i=RUN),
                in1=inverse_rows[c, i0][:, first : first + count]
                .rearrange("p (b i) -> p b i", i=RUN)
                .unsqueeze(2)
                .to_broadcast([P, count // RUN, PACK, RUN]),
                op=ALU.mult,
            )

        def quantise_x(c, i0, n, g):
            words = of_block(x_words, c, packed, [P, PASSES, BLOCK], U32, "x_words")
            planes = of_block(x_planes, c, packed, [P, PASSES, BLOCK], U8, "x_planes")
            nc.vector.quantize_mx(
                out=words[:, g, i0 * P : (i0 + n) * P].bitcast(FP8X4),
                scales=planes[:, g, i0 * P : (i0 + n) * P],
                in_=xn[c][:, g, i0 * P : (i0 + n) * P, :].rearrange("p x t -> p (x t)"),
            )

        def product_1(c, i0, n, u):
            slots = TILES // n
            h_sums[c, i0, u] = psum_h.tile([P, slots, n * P], F32, name="h_sums")
            for s in range(slots):
                t = u * slots + s
                for g in range(PASSES):
                    nc.tensor.matmul_mx(
                        out=h_sums[c, i0, u][:, s, :],
                        lhsT=w1_words[:, g, t * P : (t + 1) * P].bitcast(FP8X4),
                        lhsT_scale=w1_planes[:, g, t * P : (t + 1) * P],
                        rhs=x_words[c][:, g, i0 * P : (i0 + n) * P].bitcast(FP8X4),
                        rhs_scale=x_planes[c][:, g, i0 * P : (i0 + n) * P],
                        start=(g == 0),
                        stop=(g == PASSES - 1),
                    )

        def relu_bank(c, i0, n, u):
            slots = TILES // n
            kept = of_block(h_slots, c, stage, [P, PACK, BLOCK], BF16, "h_slots")
            for s in range(slots):
                t = u * slots + s
                nc.scalar.activation(
                    out=kept[:, t, i0 * P : (i0 + n) * P],
                    in_=h_sums[c, i0, u][:, s, :],
                    func=ACT.Relu,
                    bias=b1_slots[:, t : t + 1],
                )

        def group_hidden(c, i):
            grouped = of_block(h_grouped, c, stage, [P, BLOCK, PACK], BF16, "h_grouped")
            if on_vector(c):
                nc.vector.tensor_copy(
                    out=grouped[:, i * P : (i + 1) * P, :],
                    in_=h_slots[c][:, :, i * P : (i + 1) * P].rearrange("p t n -> p n t"),
                )
            else:
                nc.gpsimd.tensor_scalar(
                    out=grouped[:, i * P : (i + 1) * P, :],
                    in0=h_slots[c][:, :, i * P : (i + 1) * P].rearrange("p t n -> p n t"),
                    scalar1=1.0,
                    scalar2=0.0,
                    op0=ALU.mult,
                    op1=ALU.add,
                )

        def quantise_h(c, i0, n):
            words = of_block(h_words, c, packed, [P, BLOCK], U32, "h_words")
            planes = of_block(h_planes, c, packed, [P, BLOCK], U8, "h_planes")
            nc.vector.quantize_mx(
                out=words[:, i0 * P : (i0 + n) * P].bitcast(FP8X4),
                scales=planes[:, i0 * P : (i0 + n) * P],
                in_=h_grouped[c][:, i0 * P : (i0 + n) * P, :].rearrange("p n t -> p (n t)"),
            )

        def product_2(c, i0, n):
            zq_sums[c, i0] = psum_z.tile([P, n, CODE], F32, name="zq_sums")
            for i in range(n):
                nc.tensor.matmul_mx(
                    out=zq_sums[c, i0][:, i, :],
                    lhsT=h_words[c][:, (i0 + i) * P : (i0 + i + 1) * P].bitcast(FP8X4),
                    lhsT_scale=h_planes[c][:, (i0 + i) * P : (i0 + i + 1) * P],
                    rhs=w2_words[:, 0, :].bitcast(FP8X4),
                    rhs_scale=w2_planes[:, 0, :],
                    start=True,
                    stop=True,
                )

        def add_bias_2(c, i0, n):
            kept = of_block(zq, c, result, [P, TILES, CODE], F32, "zq")
            nc.vector.tensor_tensor(
                out=kept[:, i0 : i0 + n, :],
                in0=zq_sums[c, i0][:],
                in1=b2_rows[:].unsqueeze(1).to_broadcast([P, n, CODE]),
                op=ALU.add,
            )

        def mean(c, i0, n):
            kept = of_block(minus_mean, c, small, [P, TILES], F32, "minus_mean")
            for i in range(i0, i0 + n):
                shares = scrap.tile([P, CODE], F32)
                nc.scalar.activation(
                    out=shares[:],
                    in_=zq[c][:, i, :],
                    func=ACT.Identity,
                    scale=-1.0 / CODE,
                    accum_out=kept[:, i : i + 1],
                )

        def sum_deviations(c, i0, n):
            first = c * TILES + i0
            for i in range(i0, i0 + n):
                dev_squares = scrap.tile([P, CODE], F32)
                nc.scalar.activation(
                    out=dev_squares[:],
                    in_=zq[c][:, i, :],
                    func=ACT.Square,
                    bias=minus_mean[c][:, i : i + 1],
                    accum_out=dev_sumsq[:, c * TILES + i : c * TILES + i + 1],
                )
            inverse = of_block(dev_inverse, c, small, [P, TILES], F32, "dev_inverse")
            inverse_root(inverse[:, i0 : i0 + n], dev_sumsq[:, first : first + n], EPS * EPS, n)

        def normalise_and_store(c, i0, n):
            kept = of_block(zc, c, result, [P, TILES, CODE], F32, "zc")
            engine = nc.vector if on_vector(c) else nc.gpsimd
            for i in range(i0, i0 + n):
                engine.tensor_scalar(
                    out=kept[:, i, :],
                    in0=zq[c][:, i, :],
                    scalar1=minus_mean[c][:, i : i + 1],
                    scalar2=dev_inverse[c][:, i : i + 1],
                    op0=ALU.add,
                    op1=ALU.mult,
                )
            first = c * BLOCK + i0 * P
            nc.sync.dma_start(
                out=out_0[first : first + n * P, :].rearrange("(i q) d -> q i d", q=P),
                in_=kept[:, i0 : i0 + n, :],
            )

        booked = []

        def book(step, rank, stage_function, *arguments):
            booked.append((step, rank, len(booked), stage_function, arguments))

        book(6, V_GROUP, reorder_weights)
        for k in range(TOKEN_TILES):
            if by_products(k):
                book(k, T_TOKENS, multiply_tokens, k)
                book(k + 2, V_FIRST, take_diagonal, k)
            else:
                book(k, T_TOKENS, transpose_tokens, k)
                book(k + 2, S_SQUARES, sum_squares, k)

        scaled_at = [0, 0]
        bank_free = group_free = bias_2_at = 0
        for c in range(BLOCKS):
            for i0, n in parts_of(c):
                step = c * TILES + i0 + n - 1
                book(step + 2, S_INVERSE, invert_norms, c, i0, n)
                step = max(step + 3, scaled_at[-2] + 1)
                book(step, T_SPREAD, spread_inverse, c, i0, n)
                step = max(step + 2, scaled_at[-1] + 1)
                count = min(n * P, 2 * P)
                pieces = [(g, first) for g in range(PASSES) for first in range(0, n * P, count)]
                for u, (g, first) in enumerate(pieces):
                    book(step + u * n // len(pieces), V_SCALE, scale_piece, c, i0, g, first, count)
                scaled_at.append(step + n - 1)
                if i0 + n == TILES and c + Z_BUFFERS < BLOCKS:
                    book(step + n - 1, V_GROUP, load_block, c + Z_BUFFERS)
                for g in range(PASSES):
                    book(step + max(1, (g + 1) * n // PASSES), V_QUANTISE, quantise_x, c, i0, n, g)
                step = max(step + n + 1, bank_free)
                for u in range(n):
                    book(step + u, T_PRODUCT_1, product_1, c, i0, n, u)
                    book(step + u + 1, S_RELU, relu_bank, c, i0, n, u)
                bank_free = step + n
                step = max(step + n + 1, group_free)
                for i in range(n):
                    book(step + i, V_GROUP if on_vector(c) else G_GROUP, group_hidden, c, i0 + i)
                group_free = step + n
                step = step + n if on_vector(c) else step + n + 1
                book(step, V_QUANTISE, quantise_h, c, i0, n)
                step = max(step + 1, bias_2_at)
                book(step, T_PRODUCT_2, product_2, c, i0, n)
                bias_2_at = step + 1
                book(step + 1, V_FIRST, add_bias_2, c, i0, n)
                book(step + 2, S_MEAN, mean, c, i0, n)
                book(step + 3, S_DEVIATIONS, sum_deviations, c, i0, n)
                book(step + 4, LAST, normalise_and_store, c, i0, n)

        for step, rank, serial, stage_function, arguments in sorted(booked):
            stage_function(*arguments)

        var_t = psum_z.tile([P, P], F32, name="zq_sums")
        nc.tensor.transpose(var_t[:], dev_sumsq[:], ident_f32[:])
        var_rows = result.tile([P, P], F32)
        nc.vector.tensor_scalar_mul(out=var_rows[:], in0=var_t[:], scalar1=1.0 / (CODE - 1))
        nc.sync.dma_start(out=out_1.rearrange("(i q) o -> i (q o)", q=P), in_=var_rows[:TOKEN_TILES, :])
